import numpy as np
import ml_dtypes


def mxq(x, axis, fmt="e4m3"):
    dtype, down = {"e4m3": (ml_dtypes.float8_e4m3fn, 7), "e5m2": (ml_dtypes.float8_e5m2, 14)}[fmt]
    v = np.moveaxis(np.asarray(x, np.float32).astype(ml_dtypes.bfloat16).astype(np.float64), axis, -1)
    blocks = v.reshape(v.shape[:-1] + (-1, 32))
    amax = np.abs(blocks).max(-1, keepdims=True)
    byte = np.maximum(np.where(amax > 0, np.frexp(amax)[1] - 1 + 127, 0) - down, 1)
    scale = np.exp2(byte - 127.0)
    codes = (blocks / scale).astype(np.float32).astype(dtype).astype(np.float64)
    return np.moveaxis((codes * scale).reshape(v.shape), -1, axis)


WIDE = False


def mx_kscale(k):
    if not WIDE:
        return np.ones(k)
    levels = np.array([10, -10, 5, -5, 0])
    a = np.random.permutation(np.resize(levels, k // 512 * 4)).reshape(k // 512, 4)
    idx = np.arange(k)
    return np.exp2(a[idx // 512, idx % 128 // 32])


BF16 = ml_dtypes.bfloat16


def bf(x):
    return np.asarray(x, np.float32).astype(BF16)


def f64(x):
    return np.asarray(x).astype(np.float64)


N, C, D, H, W, NHEADS, KSIZE = 2, 512, 256, 32, 32, 8, 5
PAD = KSIZE // 2
HD = D // NHEADS
WIN = KSIZE * KSIZE


def _patches(t):
    tp = np.pad(t, ((0, 0), (0, 0), (PAD, PAD), (PAD, PAD)))
    return np.stack([tp[:, :, i:i + H, j:j + W] for i in range(KSIZE) for j in range(KSIZE)], axis=2)


def setup_inputs():
    s = mx_kscale(C)
    a = np.sqrt(1.5) / HD ** 0.25
    g = np.concatenate([np.full(2 * D, a), np.ones(D)])
    return {"x": bf(np.random.standard_normal((N, C, H, W)) * s[None, :, None, None]),
            "w_qkv": bf(np.random.standard_normal((3 * D, C)) * g[:, None] / np.sqrt(C) / s[None, :])}


def reference(x, w_qkv):
    xq = mxq(f64(x).reshape(N, C, H * W), 1, "e4m3")
    wq = mxq(f64(w_qkv), 1, "e4m3")
    qkv = (wq @ xq).reshape(N, 3 * D, H, W)
    Q, K, V = np.split(qkv, 3, axis=1)
    Qh = Q.reshape(N, NHEADS, HD, 1, H, W)
    scores = np.sum(_patches(K).reshape(N, NHEADS, HD, WIN, H, W) * Qh, axis=2, keepdims=True)
    e = np.exp(scores - scores.max(axis=3, keepdims=True))
    att = e / e.sum(axis=3, keepdims=True)
    out = np.sum(_patches(V).reshape(N, NHEADS, HD, WIN, H, W) * att, axis=3).reshape(N, D, H, W)
    return out

@@ -1,0 +1,280 @@
+from contextlib import ExitStack
+
+import concourse.mybir as mybir
+from concourse.masks import make_identity
+
+F32 = mybir.dt.float32
+BF16 = mybir.dt.bfloat16
+U32 = mybir.dt.uint32
+U8 = mybir.dt.uint8
+FP8X4 = mybir.dt.float8_e4m3fn_x4
+ALU = mybir.AluOpType
+ACT = mybir.ActivationFunctionType
+AX = mybir.AxisListType
+
+P = 128
+FLOPS = 2 * 768 * 512 * 2048 + 2 * 2 * 2048 * 8 * 25 * 32
+
+VECTOR_PIECES = (
+    (),
+    (),
+    tuple(range(20)),
+    (0, 2, 4, 6, 8, 10, 12, 14, 16, 18, 19),
+)
+
+
+def tile_relation_kernel(tc, x, w_qkv, out):
+    nc = tc.nc
+    with ExitStack() as ctx:
+        keep = ctx.enter_context(tc.tile_pool(name="keep", bufs=1))
+        ring = ctx.enter_context(tc.tile_pool(name="ring", bufs=4))
+        soft = ctx.enter_context(tc.tile_pool(name="soft", bufs=2))
+        psum = ctx.enter_context(tc.psum_pool(name="psum", bufs=2))
+
+        ident_f = keep.tile([P, P], F32, name="ident_f")
+        make_identity(nc, ident_f[:])
+        ident_b = keep.tile([P, P], BF16, name="ident_b")
+        make_identity(nc, ident_b[:])
+        wc = keep.tile([P, 768], U32, name="wc", align_bytes=64)
+        ws = keep.tile([P, 768], U8, name="ws", align_bytes=64)
+        q_rows = [keep.tile([P, 32, 32], F32, name="q%d" % r) for r in range(4)]
+        k_rows = [keep.tile([P, 32, 64], F32, name="k%d" % r) for r in range(8)]
+        v_rows = [keep.tile([P, 8, 8, 32], F32, name="v%d" % r) for r in range(8)]
+
+        wraw = ring.tile([P, 6, 512], BF16, name="wraw", tag="b8", align_bytes=64)
+        nc.sync.dma_start(out=wraw[:], in_=w_qkv.rearrange("(r p) k -> p r k", p=P))
+        raws = []
+        for n in range(2):
+            raw = ring.tile([P, 4, 1024], BF16, name="raw%d" % n, tag="b8", align_bytes=64)
+            nc.sync.dma_start(out=raw[:], in_=x[n].rearrange("(t p) h w -> p t (h w)", p=P))
+            raws.append(raw)
+
+        wgrp = ring.tile([P, 768, 4], BF16, name="wgrp", tag="b8", align_bytes=64)
+        for r in range(6):
+            ty, hh = divmod(r, 2)
+            wt = psum.tile([P, 4, P], BF16, name="wt", tag="w", bufs=4)
+            for t in range(4):
+                nc.tensor.transpose(wt[:, t, :], wraw[:, r, P * t : P * (t + 1)], ident_b[:])
+            if ty < 2:
+                dst = wgrp[:, 256 * ty : 256 * (ty + 1), :].rearrange("p (c h) t -> p c h t", h=8)
+                dst = dst[:, :, 4 * hh : 4 * (hh + 1), :]
+                src = wt[:].rearrange("p t (h c) -> p c h t", c=32)
+            else:
+                dst = wgrp[:, 512 + P * hh : 512 + P * (hh + 1), :]
+                src = wt[:].rearrange("p t r -> p r t")
+            if r % 2 == 0:
+                nc.vector.tensor_copy(out=dst, in_=src)
+            else:
+                nc.scalar.copy(out=dst, in_=src)
+        for ty in range(3):
+            cols = slice(256 * ty, 256 * (ty + 1))
+            nc.vector.quantize_mx(
+                out=wc[:, cols].bitcast(FP8X4),
+                scales=ws[:, cols],
+                in_=wgrp[:, cols, :].rearrange("p w t -> p (w t)"),
+            )
+
+        inters = []
+        for n in range(2):
+            inter = ring.tile([P, 1024, 4], BF16, name="inter%d" % n, tag="b8", align_bytes=64)
+            for eng, lo, hi in ((nc.vector.tensor_copy, 0, 640), (nc.scalar.copy, 640, 1024)):
+                eng(
+                    out=inter[:, lo:hi, :].rearrange("p (c i) t -> p c t i", i=4),
+                    in_=raws[n][:, :, lo:hi].rearrange("p t (c i) -> p c t i", i=4),
+                )
+            inters.append(
+                inter[:]
+                .rearrange("p x t -> p (x t)")
+                .bitcast(F32)
+                .rearrange("p (hb hl wb wl u) -> p hb hl wb wl u", hb=8, hl=4, wb=8, wl=4)
+            )
+
+        with tc.tile_pool(name="codes", bufs=1) as codes:
+            xc = []
+            xs = []
+            for a in range(8):
+                grp = ring.tile([P, 4096], BF16, name="grp", tag="b8", align_bytes=64)
+                g_f = grp[:].bitcast(F32).rearrange("p (b n hb wb u) -> p b n hb wb u", b=8, n=2, hb=8, wb=8)
+                nc.vector.memset(g_f[:, 0:2, :, :, 0, :], 0.0)
+                nc.vector.memset(g_f[:, 6:8, :, :, 7, :], 0.0)
+                if a < 2:
+                    nc.vector.memset(g_f[:, :, :, 0, :, :], 0.0)
+                    hl_src, hd, hs = a + 2, slice(1, 8), slice(0, 7)
+                elif a < 6:
+                    hl_src, hd, hs = a - 2, slice(0, 8), slice(0, 8)
+                else:
+                    nc.vector.memset(g_f[:, :, :, 7, :, :], 0.0)
+                    hl_src, hd, hs = a - 6, slice(0, 7), slice(1, 8)
+                for n in range(2):
+                    for bs, wls, wd, wsrc in (
+                        (slice(0, 2), slice(2, 4), slice(1, 8), slice(0, 7)),
+                        (slice(2, 6), slice(0, 4), slice(0, 8), slice(0, 8)),
+                        (slice(6, 8), slice(0, 2), slice(0, 7), slice(1, 8)),
+                    ):
+                        nc.vector.tensor_copy(
+                            out=g_f[:, bs, n, hd, wd, :],
+                            in_=inters[n][:, hs, hl_src, wsrc, wls, :].rearrange("p hb wb wl u -> p wl hb wb u"),
+                        )
+                xc_a = codes.tile([P, 1024], U32, name="xc%d" % a, align_bytes=64)
+                xs_a = codes.tile([P, 1024], U8, name="xs%d" % a, align_bytes=64)
+                nc.vector.quantize_mx(out=xc_a[:].bitcast(FP8X4), scales=xs_a[:], in_=grp[:])
+                xc.append(xc_a)
+                xs.append(xs_a)
+
+                jobs = [(1, b0, k_rows[a][:, :, 8 * b0 : 8 * (b0 + 2)]) for b0 in (0, 2, 4, 6)]
+                if 2 <= a < 6:
+                    jobs += [(0, b0, q_rows[a - 2][:, :, 8 * (b0 - 2) : 8 * b0]) for b0 in (2, 4)]
+                for ty, b0, dst in jobs:
+                    ps = psum.tile([P, 2, 256], F32, name="ps", tag="w", bufs=4)
+                    for u in range(2):
+                        cols = slice(P * (b0 + u), P * (b0 + u + 1))
+                        nc.tensor.matmul_mx(
+                            out=ps[:, u, :],
+                            lhsT=xc_a[:, cols].bitcast(FP8X4),
+                            lhsT_scale=xs_a[:, cols],
+                            rhs=wc[:, 256 * ty : 256 * (ty + 1)].bitcast(FP8X4),
+                            rhs_scale=ws[:, 256 * ty : 256 * (ty + 1)],
+                            start=True,
+                            stop=True,
+                        )
+                    nc.scalar.copy(
+                        out=dst.rearrange("p c (u h) -> p c u h", h=8),
+                        in_=ps[:].rearrange("p u (c h) -> p c u h", h=8),
+                    )
+            for a in range(8):
+                for b0 in (0, 2, 4, 6):
+                    ps = psum.tile([P, 2, 256], F32, name="ps", tag="w", bufs=4)
+                    for u in range(2):
+                        cols = slice(P * (b0 + u), P * (b0 + u + 1))
+                        nc.tensor.matmul_mx(
+                            out=ps[:, u, :],
+                            lhsT=xc[a][:, cols].bitcast(FP8X4),
+                            lhsT_scale=xs[a][:, cols],
+                            rhs=wc[:, 512:768].bitcast(FP8X4),
+                            rhs_scale=ws[:, 512:768],
+                            start=True,
+                            stop=True,
+                        )
+                    nc.scalar.copy(
+                        out=v_rows[a][:, b0 : b0 + 2, :, :].rearrange("p b h c -> p b (h c)"),
+                        in_=ps[:],
+                    )
+
+        with tc.tile_pool(name="late", bufs=4) as late:
+
+            def softmax(ssb):
+                mx = soft.tile([P, 32], F32, name="mx", tag="mx")
+                nc.vector.tensor_reduce(out=mx[:], in_=ssb[:].rearrange("p o f -> p f o"), axis=AX.X, op=ALU.max)
+                nmx = soft.tile([P, 32], F32, name="nmx", tag="nmx")
+                nc.vector.tensor_scalar(out=nmx[:], in0=mx[:], scalar1=-1.0, scalar2=None, op0=ALU.mult)
+                e = late.tile([P, 32, 25], F32, name="e", tag="e")
+                ssum = soft.tile([P, 32], F32, name="ssum", tag="ssum")
+                for f in range(32):
+                    nc.scalar.activation(
+                        out=e[:, f, :],
+                        in_=ssb[:, :, f],
+                        func=ACT.Exp,
+                        bias=nmx[:, f : f + 1],
+                        scale=1.0,
+                        accum_out=ssum[:, f : f + 1],
+                    )
+                rs = soft.tile([P, 32], F32, name="rs", tag="rs")
+                nc.vector.reciprocal(out=rs[:], in_=ssum[:])
+                nc.vector.tensor_tensor(
+                    out=e[:], in0=e[:], in1=rs[:].unsqueeze(2).to_broadcast([P, 32, 25]), op=ALU.mult
+                )
+                return e
+
+            def weighted_sum(g, e):
+                ots = [psum.tile([P, 512], F32, name="ot%d" % half, tag="w", bufs=4) for half in range(2)]
+                for wl in range(4):
+                    for i in range(5):
+                        tmp = late.tile([P, 5, 8, 32], F32, name="tmp", tag="tmp")
+                        if wl * 5 + i in VECTOR_PIECES[g]:
+                            nc.vector.tensor_tensor(
+                                out=tmp[:],
+                                in0=v_rows[g + i][:, wl : wl + 5, :, :],
+                                in1=e[:, 8 * wl : 8 * (wl + 1), 5 * i : 5 * (i + 1)]
+                                .rearrange("p h j -> p j h")
+                                .unsqueeze(3)
+                                .to_broadcast([P, 5, 8, 32]),
+                                op=ALU.mult,
+                            )
+                        else:
+                            for j in range(5):
+                                for h in range(8):
+                                    nc.scalar.activation(
+                                        out=tmp[:, j, h, :],
+                                        in_=v_rows[g + i][:, wl + j, h, :],
+                                        func=ACT.Copy,
+                                        scale=e[:, 8 * wl + h, 5 * i + j : 5 * i + j + 1],
+                                    )
+                        for j in range(5):
+                            for half in range(2):
+                                nc.tensor.matmul(
+                                    out=ots[half][:, P * wl : P * (wl + 1)],
+                                    lhsT=tmp[:, j, 4 * half : 4 * (half + 1), :].rearrange("p h c -> p (h c)"),
+                                    rhs=ident_f[:],
+                                    is_transpose=True,
+                                    start=(i == 0 and j == 0),
+                                    stop=(i == 4 and j == 4),
+                                )
+                for half in range(2):
+                    ost = late.tile([P, 16, 8, 4], F32, name="ost", tag="ost", bufs=2)
+                    src = ots[half][:].rearrange("c (wl m wb) -> c m wb wl", wl=4, wb=8)
+                    if half == 0:
+                        nc.vector.tensor_copy(out=ost[:], in_=src)
+                    else:
+                        nc.scalar.copy(out=ost[:], in_=src)
+                    for n in range(2):
+                        nc.sync.dma_start(
+                            out=out[n, P * half : P * (half + 1)].rearrange("c (hb hl) w -> c hb hl w", hl=4)[:, :, g, :],
+                            in_=ost[:, 8 * n : 8 * (n + 1)].rearrange("c m wb wl -> c m (wb wl)"),
+                        )
+
+            ssbs = {}
+            late_groups = []
+            for k in range(25):
+                st = psum.tile([P, P], F32, name="st", tag="st", bufs=2)
+                for ch in range(2):
+                    cs = slice(16 * ch, 16 * (ch + 1))
+                    pr = ring.tile([P, 16, 4, 32], F32, name="pr", tag="b8", align_bytes=64)
+                    for s in range(4):
+                        g, o = divmod(4 * k + s, 25)
+                        i, j = divmod(o, 5)
+                        nc.vector.tensor_tensor(
+                            out=pr[:, :, s, :],
+                            in0=q_rows[g][:, cs, :],
+                            in1=k_rows[g + i][:, cs, 8 * j : 8 * j + 32],
+                            op=ALU.mult,
+                        )
+                    for c in range(16):
+                        nc.tensor.matmul(
+                            out=st[:],
+                            lhsT=pr[:, c, :, :].rearrange("p s f -> p (s f)"),
+                            rhs=ident_f[:],
+                            is_transpose=True,
+                            start=(ch == 0 and c == 0),
+                            stop=(ch == 1 and c == 15),
+                        )
+                stsb = soft.tile([P, P], F32, name="stsb", tag="stsb")
+                nc.scalar.copy(out=stsb[:], in_=st[:])
+                sbp = psum.tile([P, 4, 32], F32, name="sbp", tag="sb", bufs=2)
+                nc.tensor.transpose(sbp[:].rearrange("p s f -> p (s f)"), stsb[:], ident_f[:])
+                for g in sorted(set((4 * k + s) // 25 for s in range(4))):
+                    slots = [s for s in range(4) if (4 * k + s) // 25 == g]
+                    o0 = 4 * k + slots[0] - 25 * g
+                    if g not in ssbs:
+                        ssbs[g] = soft.tile([P, 25, 32], F32, name="ssb", tag="ssb")
+                    nc.scalar.copy(
+                        out=ssbs[g][:, o0 : o0 + len(slots), :],
+                        in_=sbp[:, slots[0] : slots[-1] + 1, :],
+                    )
+                    if o0 + len(slots) == 25:
+                        e = softmax(ssbs[g])
+                        if len(VECTOR_PIECES[g]) < 10:
+                            weighted_sum(g, e)
+                        else:
+                            late_groups.append((g, e))
+            for g, e in late_groups:
+                weighted_sum(g, e)

@@ -15,19 +15,18 @@ AX = mybir.AxisListType
 P = 128
 FLOPS = 2 * 768 * 512 * 2048 + 2 * 2 * 2048 * 8 * 25 * 32
 
-VECTOR_PIECES = (
-    (),
-    (),
-    tuple(range(20)),
-    (0, 2, 4, 6, 8, 10, 12, 14, 16, 18, 19),
-)
+N_CHUNKS = 25
+VECTOR_REDUCED = (5, 6, 11, 12, 17, 18, 23, 24)
+WARMERS = 0
+VECTOR_OFFSETS = 13
 
 
 def tile_relation_kernel(tc, x, w_qkv, out):
     nc = tc.nc
     with ExitStack() as ctx:
+        ctx.enter_context(tc.manual_schedule())
         keep = ctx.enter_context(tc.tile_pool(name="keep", bufs=1))
-        ring = ctx.enter_context(tc.tile_pool(name="ring", bufs=4))
+        ring = ctx.enter_context(tc.tile_pool(name="ring", bufs=5))
         soft = ctx.enter_context(tc.tile_pool(name="soft", bufs=2))
         psum = ctx.enter_context(tc.psum_pool(name="psum", bufs=2))
 
@@ -37,22 +36,37 @@ def tile_relation_kernel(tc, x, w_qkv, out):
         make_identity(nc, ident_b[:])
         wc = keep.tile([P, 768], U32, name="wc", align_bytes=64)
         ws = keep.tile([P, 768], U8, name="ws", align_bytes=64)
-        q_rows = [keep.tile([P, 32, 32], F32, name="q%d" % r) for r in range(4)]
         k_rows = [keep.tile([P, 32, 64], F32, name="k%d" % r) for r in range(8)]
         v_rows = [keep.tile([P, 8, 8, 32], F32, name="v%d" % r) for r in range(8)]
+        core_c = [keep.tile([P, 512], U32, name="cc%d" % r, align_bytes=64) for r in range(4)]
+        core_s = [keep.tile([P, 512], U8, name="cs%d" % r, align_bytes=64) for r in range(4)]
 
-        wraw = ring.tile([P, 6, 512], BF16, name="wraw", tag="b8", align_bytes=64)
+        def ring_tile(shape, dtype, name):
+            return ring.tile(shape, dtype, name=name, tag="b8", align_bytes=64)
+
+        def project(dst, codes, scales, lo, hi):
+            nc.tensor.matmul_mx(
+                out=dst,
+                lhsT=codes.bitcast(FP8X4),
+                lhsT_scale=scales,
+                rhs=wc[:, lo:hi].bitcast(FP8X4),
+                rhs_scale=ws[:, lo:hi],
+                start=True,
+                stop=True,
+            )
+
+        wraw = ring_tile([P, 6, 512], BF16, "wraw")
         nc.sync.dma_start(out=wraw[:], in_=w_qkv.rearrange("(r p) k -> p r k", p=P))
         raws = []
         for n in range(2):
-            raw = ring.tile([P, 4, 1024], BF16, name="raw%d" % n, tag="b8", align_bytes=64)
+            raw = ring_tile([P, 4, 1024], BF16, "raw%d" % n)
             nc.sync.dma_start(out=raw[:], in_=x[n].rearrange("(t p) h w -> p t (h w)", p=P))
             raws.append(raw)
 
-        wgrp = ring.tile([P, 768, 4], BF16, name="wgrp", tag="b8", align_bytes=64)
+        wgrp = ring_tile([P, 768, 4], BF16, "wgrp")
         for r in range(6):
             ty, hh = divmod(r, 2)
-            wt = psum.tile([P, 4, P], BF16, name="wt", tag="w", bufs=4)
+            wt = psum.tile([P, 4, P], BF16, name="wt", tag="w", bufs=2)
             for t in range(4):
                 nc.tensor.transpose(wt[:, t, :], wraw[:, r, P * t : P * (t + 1)], ident_b[:])
             if ty < 2:
@@ -66,17 +80,10 @@ def tile_relation_kernel(tc, x, w_qkv, out):
                 nc.vector.tensor_copy(out=dst, in_=src)
             else:
                 nc.scalar.copy(out=dst, in_=src)
-        for ty in range(3):
-            cols = slice(256 * ty, 256 * (ty + 1))
-            nc.vector.quantize_mx(
-                out=wc[:, cols].bitcast(FP8X4),
-                scales=ws[:, cols],
-                in_=wgrp[:, cols, :].rearrange("p w t -> p (w t)"),
-            )
 
         inters = []
         for n in range(2):
-            inter = ring.tile([P, 1024, 4], BF16, name="inter%d" % n, tag="b8", align_bytes=64)
+            inter = ring_tile([P, 1024, 4], BF16, "inter%d" % n)
             for eng, lo, hi in ((nc.vector.tensor_copy, 0, 640), (nc.scalar.copy, 640, 1024)):
                 eng(
                     out=inter[:, lo:hi, :].rearrange("p (c i) t -> p c t i", i=4),
@@ -88,140 +95,250 @@ def tile_relation_kernel(tc, x, w_qkv, out):
                 .bitcast(F32)
                 .rearrange("p (hb hl wb wl u) -> p hb hl wb wl u", hb=8, hl=4, wb=8, wl=4)
             )
-
-        with tc.tile_pool(name="codes", bufs=1) as codes:
-            xc = []
-            xs = []
-            for a in range(8):
-                grp = ring.tile([P, 4096], BF16, name="grp", tag="b8", align_bytes=64)
-                g_f = grp[:].bitcast(F32).rearrange("p (b n hb wb u) -> p b n hb wb u", b=8, n=2, hb=8, wb=8)
-                nc.vector.memset(g_f[:, 0:2, :, :, 0, :], 0.0)
-                nc.vector.memset(g_f[:, 6:8, :, :, 7, :], 0.0)
-                if a < 2:
-                    nc.vector.memset(g_f[:, :, :, 0, :, :], 0.0)
-                    hl_src, hd, hs = a + 2, slice(1, 8), slice(0, 7)
-                elif a < 6:
-                    hl_src, hd, hs = a - 2, slice(0, 8), slice(0, 8)
-                else:
-                    nc.vector.memset(g_f[:, :, :, 7, :, :], 0.0)
-                    hl_src, hd, hs = a - 6, slice(0, 7), slice(1, 8)
-                for n in range(2):
-                    for bs, wls, wd, wsrc in (
-                        (slice(0, 2), slice(2, 4), slice(1, 8), slice(0, 7)),
-                        (slice(2, 6), slice(0, 4), slice(0, 8), slice(0, 8)),
-                        (slice(6, 8), slice(0, 2), slice(0, 7), slice(1, 8)),
-                    ):
-                        nc.vector.tensor_copy(
-                            out=g_f[:, bs, n, hd, wd, :],
-                            in_=inters[n][:, hs, hl_src, wsrc, wls, :].rearrange("p hb wb wl u -> p wl hb wb u"),
-                        )
-                xc_a = codes.tile([P, 1024], U32, name="xc%d" % a, align_bytes=64)
-                xs_a = codes.tile([P, 1024], U8, name="xs%d" % a, align_bytes=64)
-                nc.vector.quantize_mx(out=xc_a[:].bitcast(FP8X4), scales=xs_a[:], in_=grp[:])
-                xc.append(xc_a)
-                xs.append(xs_a)
-
-                jobs = [(1, b0, k_rows[a][:, :, 8 * b0 : 8 * (b0 + 2)]) for b0 in (0, 2, 4, 6)]
-                if 2 <= a < 6:
-                    jobs += [(0, b0, q_rows[a - 2][:, :, 8 * (b0 - 2) : 8 * b0]) for b0 in (2, 4)]
-                for ty, b0, dst in jobs:
-                    ps = psum.tile([P, 2, 256], F32, name="ps", tag="w", bufs=4)
-                    for u in range(2):
-                        cols = slice(P * (b0 + u), P * (b0 + u + 1))
-                        nc.tensor.matmul_mx(
-                            out=ps[:, u, :],
-                            lhsT=xc_a[:, cols].bitcast(FP8X4),
-                            lhsT_scale=xs_a[:, cols],
-                            rhs=wc[:, 256 * ty : 256 * (ty + 1)].bitcast(FP8X4),
-                            rhs_scale=ws[:, 256 * ty : 256 * (ty + 1)],
-                            start=True,
-                            stop=True,
-                        )
-                    nc.scalar.copy(
-                        out=dst.rearrange("p c (u h) -> p c u h", h=8),
-                        in_=ps[:].rearrange("p u (c h) -> p c u h", h=8),
-                    )
-            for a in range(8):
-                for b0 in (0, 2, 4, 6):
-                    ps = psum.tile([P, 2, 256], F32, name="ps", tag="w", bufs=4)
-                    for u in range(2):
-                        cols = slice(P * (b0 + u), P * (b0 + u + 1))
-                        nc.tensor.matmul_mx(
-                            out=ps[:, u, :],
-                            lhsT=xc[a][:, cols].bitcast(FP8X4),
-                            lhsT_scale=xs[a][:, cols],
-                            rhs=wc[:, 512:768].bitcast(FP8X4),
-                            rhs_scale=ws[:, 512:768],
-                            start=True,
-                            stop=True,
-                        )
-                    nc.scalar.copy(
-                        out=v_rows[a][:, b0 : b0 + 2, :, :].rearrange("p b h c -> p b (h c)"),
-                        in_=ps[:],
+            if n == 0:
+                for ty in range(3):
+                    cols = slice(256 * ty, 256 * (ty + 1))
+                    nc.vector.quantize_mx(
+                        out=wc[:, cols].bitcast(FP8X4),
+                        scales=ws[:, cols],
+                        in_=wgrp[:, cols, :].rearrange("p w t -> p (w t)"),
                     )
 
-        with tc.tile_pool(name="late", bufs=4) as late:
+        tiles = {}
 
-            def softmax(ssb):
-                mx = soft.tile([P, 32], F32, name="mx", tag="mx")
-                nc.vector.tensor_reduce(out=mx[:], in_=ssb[:].rearrange("p o f -> p f o"), axis=AX.X, op=ALU.max)
-                nmx = soft.tile([P, 32], F32, name="nmx", tag="nmx")
-                nc.vector.tensor_scalar(out=nmx[:], in0=mx[:], scalar1=-1.0, scalar2=None, op0=ALU.mult)
-                e = late.tile([P, 32, 25], F32, name="e", tag="e")
-                ssum = soft.tile([P, 32], F32, name="ssum", tag="ssum")
-                for f in range(32):
-                    nc.scalar.activation(
-                        out=e[:, f, :],
-                        in_=ssb[:, :, f],
-                        func=ACT.Exp,
-                        bias=nmx[:, f : f + 1],
-                        scale=1.0,
-                        accum_out=ssum[:, f : f + 1],
+        def gather_row(a):
+            grp = ring_tile([P, 4096], BF16, "grp")
+            g_f = grp[:].bitcast(F32).rearrange("p (b n hb wb u) -> p b n hb wb u", b=8, n=2, hb=8, wb=8)
+            nc.vector.memset(g_f[:, 0:2, :, :, 0, :], 0.0)
+            nc.vector.memset(g_f[:, 6:8, :, :, 7, :], 0.0)
+            if a < 2:
+                nc.vector.memset(g_f[:, :, :, 0, :, :], 0.0)
+                hl_src, hd, hs = a + 2, slice(1, 8), slice(0, 7)
+            elif a < 6:
+                hl_src, hd, hs = a - 2, slice(0, 8), slice(0, 8)
+            else:
+                nc.vector.memset(g_f[:, :, :, 7, :, :], 0.0)
+                hl_src, hd, hs = a - 6, slice(0, 7), slice(1, 8)
+            for n in range(2):
+                for bs, wls, wd, wsrc in (
+                    (slice(0, 2), slice(2, 4), slice(1, 8), slice(0, 7)),
+                    (slice(2, 6), slice(0, 4), slice(0, 8), slice(0, 8)),
+                    (slice(6, 8), slice(0, 2), slice(0, 7), slice(1, 8)),
+                ):
+                    nc.vector.tensor_copy(
+                        out=g_f[:, bs, n, hd, wd, :],
+                        in_=inters[n][:, hs, hl_src, wsrc, wls, :].rearrange("p hb wb wl u -> p wl hb wb u"),
                     )
-                rs = soft.tile([P, 32], F32, name="rs", tag="rs")
-                nc.vector.reciprocal(out=rs[:], in_=ssum[:])
-                nc.vector.tensor_tensor(
-                    out=e[:], in0=e[:], in1=rs[:].unsqueeze(2).to_broadcast([P, 32, 25]), op=ALU.mult
+            return grp
+
+        def quantise_row(codes, a, grp):
+            if 2 <= a < 6:
+                hc = codes.tile([P, 512], U32, name="hc%d" % a, align_bytes=64)
+                hs_ = codes.tile([P, 512], U8, name="hs%d" % a, align_bytes=64)
+                parts = (
+                    (0, 2, hc[:, 0:256], hs_[:, 0:256]),
+                    (2, 6, core_c[a - 2][:], core_s[a - 2][:]),
+                    (6, 8, hc[:, 256:512], hs_[:, 256:512]),
                 )
-                return e
+            else:
+                hc = codes.tile([P, 1024], U32, name="hc%d" % a, align_bytes=64)
+                hs_ = codes.tile([P, 1024], U8, name="hs%d" % a, align_bytes=64)
+                parts = ((0, 8, hc[:], hs_[:]),)
+            for b0, b1, c_ap, s_ap in parts:
+                nc.vector.quantize_mx(out=c_ap.bitcast(FP8X4), scales=s_ap, in_=grp[:, 512 * b0 : 512 * b1])
+                for b in range(b0, b1):
+                    tiles[(a, b)] = (c_ap[:, P * (b - b0) : P * (b - b0 + 1)], s_ap[:, P * (b - b0) : P * (b - b0 + 1)])
 
-            def weighted_sum(g, e):
-                ots = [psum.tile([P, 512], F32, name="ot%d" % half, tag="w", bufs=4) for half in range(2)]
-                for wl in range(4):
-                    for i in range(5):
-                        tmp = late.tile([P, 5, 8, 32], F32, name="tmp", tag="tmp")
-                        if wl * 5 + i in VECTOR_PIECES[g]:
-                            nc.vector.tensor_tensor(
-                                out=tmp[:],
-                                in0=v_rows[g + i][:, wl : wl + 5, :, :],
-                                in1=e[:, 8 * wl : 8 * (wl + 1), 5 * i : 5 * (i + 1)]
-                                .rearrange("p h j -> p j h")
-                                .unsqueeze(3)
-                                .to_broadcast([P, 5, 8, 32]),
-                                op=ALU.mult,
-                            )
-                        else:
-                            for j in range(5):
-                                for h in range(8):
-                                    nc.scalar.activation(
-                                        out=tmp[:, j, h, :],
-                                        in_=v_rows[g + i][:, wl + j, h, :],
-                                        func=ACT.Copy,
-                                        scale=e[:, 8 * wl + h, 5 * i + j : 5 * i + j + 1],
-                                    )
-                        for j in range(5):
-                            for half in range(2):
-                                nc.tensor.matmul(
-                                    out=ots[half][:, P * wl : P * (wl + 1)],
-                                    lhsT=tmp[:, j, 4 * half : 4 * (half + 1), :].rearrange("p h c -> p (h c)"),
-                                    rhs=ident_f[:],
-                                    is_transpose=True,
-                                    start=(i == 0 and j == 0),
-                                    stop=(i == 4 and j == 4),
-                                )
+        def k_row(a):
+            for b0 in (0, 2, 4, 6):
+                ps = psum.tile([P, 2, 256], F32, name="ps", tag="w", bufs=2)
+                for u in range(2):
+                    project(ps[:, u, :], tiles[(a, b0 + u)][0], tiles[(a, b0 + u)][1], 256, 512)
+                nc.scalar.copy(
+                    out=k_rows[a][:, :, 8 * b0 : 8 * (b0 + 2)].rearrange("p c (u h) -> p c u h", h=8),
+                    in_=ps[:].rearrange("p u (c h) -> p c u h", h=8),
+                )
+
+        def v_row(a):
+            for b0 in (0, 2, 4, 6):
+                ps = psum.tile([P, 2, 256], F32, name="ps", tag="w", bufs=2)
+                for u in range(2):
+                    project(ps[:, u, :], tiles[(a, b0 + u)][0], tiles[(a, b0 + u)][1], 512, 768)
+                nc.scalar.copy(out=v_rows[a][:, b0 : b0 + 2, :, :].rearrange("p b h c -> p b (h c)"), in_=ps[:])
+
+        q_banks = {}
+
+        def q_bank(g, ch):
+            qp = psum.tile([P, 4, 16, 8], F32, name="qp", tag="qp", bufs=3)
+            for wl in range(4):
+                project(
+                    qp[:, wl, :, :].rearrange("p c h -> p (c h)"),
+                    tiles[(g + 2, wl + 2)][0],
+                    tiles[(g + 2, wl + 2)][1],
+                    P * ch,
+                    P * (ch + 1),
+                )
+            q_banks[(g, ch)] = qp
+
+        def groups_of(k):
+            return sorted(set((4 * k + s) // 25 for s in range(4)))
+
+        halves = {}
+
+        def products(k, ch):
+            cs = slice(16 * ch, 16 * (ch + 1))
+            pr = ring_tile([P, 16, 4, 32], F32, "pr")
+            for s in range(4):
+                g, o = divmod(4 * k + s, 25)
+                i, j = divmod(o, 5)
+                nc.vector.tensor_tensor(
+                    out=pr[:, :, s, :].rearrange("p c (wl h) -> p c wl h", h=8),
+                    in0=q_banks[(g, ch)][:].rearrange("p wl c h -> p c wl h"),
+                    in1=k_rows[g + i][:, cs, 8 * j : 8 * j + 32].rearrange("p c (wl h) -> p c wl h", h=8),
+                    op=ALU.mult,
+                )
+            halves[(k, ch)] = pr
+
+        def fold(k):
+            a_ap = halves[(k, 0)][:].rearrange("p c s f -> p (c s f)")
+            nc.gpsimd.tensor_tensor(
+                out=a_ap, in0=a_ap, in1=halves[(k, 1)][:].rearrange("p c s f -> p (c s f)"), op=ALU.add
+            )
+
+        ssbs = {}
+
+        def score_parts(k):
+            parts = []
+            for g in groups_of(k):
+                slots = [s for s in range(4) if (4 * k + s) // 25 == g]
+                if g not in ssbs:
+                    ssbs[g] = soft.tile([P, 25, 32], F32, name="ssb", tag="ssb")
+                o0 = 4 * k + slots[0] - 25 * g
+                parts.append((ssbs[g][:, o0 : o0 + len(slots), :], slots[0], slots[-1] + 1))
+            return parts
+
+        def vector_reduce(k):
+            for dst, s0, s1 in score_parts(k):
+                nc.vector.tensor_reduce(
+                    out=dst, in_=halves[(k, 0)][:, :, s0:s1, :].rearrange("p c s f -> p s f c"), axis=AX.X, op=ALU.add
+                )
+
+        sts = {}
+
+        def warm(n):
+            for r in range(n):
+                dm = psum.tile([P, 512], F32, name="dm", tag="dm", bufs=1)
+                project(dm[:], wc[:, 0:P], ws[:, 0:P], 256, 768)
+
+        def tensor_reduce(k):
+            st = psum.tile([P, P], F32, name="st", tag="st", bufs=2)
+            for c in range(16):
+                nc.tensor.matmul(
+                    out=st[:],
+                    lhsT=halves[(k, 0)][:, c, :, :].rearrange("p s f -> p (s f)"),
+                    rhs=ident_f[:],
+                    is_transpose=True,
+                    start=(c == 0),
+                    stop=(c == 15),
+                )
+            sts[k] = st
+
+        def copy_st(k):
+            stsb = soft.tile([P, P], F32, name="stsb", tag="stsb")
+            nc.scalar.copy(out=stsb[:], in_=sts[k][:])
+            sts[k] = stsb
+
+        def back(k):
+            sbp = psum.tile([P, 4, 32], F32, name="sbp", tag="st", bufs=2)
+            nc.tensor.transpose(sbp[:].rearrange("p s f -> p (s f)"), sts[k][:], ident_f[:])
+            sts[k] = sbp
+
+        def copy_back(k):
+            for dst, s0, s1 in score_parts(k):
+                nc.scalar.copy(out=dst, in_=sts[k][:, s0:s1, :])
+
+        nmxs = {}
+        es = {}
+        sums = {}
+
+        def softmax_max(g):
+            mx = soft.tile([P, 32], F32, name="mx", tag="mx")
+            nc.vector.tensor_reduce(out=mx[:], in_=ssbs[g][:].rearrange("p o f -> p f o"), axis=AX.X, op=ALU.max)
+            nmx = soft.tile([P, 32], F32, name="nmx", tag="nmx")
+            nc.vector.tensor_scalar(out=nmx[:], in0=mx[:], scalar1=-1.0, scalar2=None, op0=ALU.mult)
+            nmxs[g] = nmx
+
+        def softmax_exp(late, g):
+            e = late.tile([P, 32, 25], F32, name="e", tag="e", bufs=3)
+            ssum = soft.tile([P, 32], F32, name="ssum", tag="ssum")
+            for f in range(32):
+                nc.scalar.activation(
+                    out=e[:, f, :],
+                    in_=ssbs[g][:, :, f],
+                    func=ACT.Exp,
+                    bias=nmxs[g][:, f : f + 1],
+                    scale=1.0,
+                    accum_out=ssum[:, f : f + 1],
+                )
+            es[g] = e
+            sums[g] = ssum
+
+        def softmax_norm(g):
+            rs = soft.tile([P, 32], F32, name="rs", tag="rs")
+            nc.vector.reciprocal(out=rs[:], in_=sums[g][:])
+            nc.vector.tensor_tensor(
+                out=es[g][:], in0=es[g][:], in1=rs[:].unsqueeze(2).to_broadcast([P, 32, 25]), op=ALU.mult
+            )
+
+        def piece_scalar(late, g, wl, offsets):
+            tmp = late.tile([P, 5, 8, 32], F32, name="tmp", tag="tmp", bufs=4)
+            for r, o in enumerate(offsets):
+                for h in range(8):
+                    nc.scalar.activation(
+                        out=tmp[:, r, h, :],
+                        in_=v_rows[g + o // 5][:, wl + o % 5, h, :],
+                        func=ACT.Copy,
+                        scale=es[g][:, 8 * wl + h, o : o + 1],
+                    )
+            return tmp
+
+        def piece_vector(late, g, wl, offsets):
+            acc = late.tile([P, 1, 8, 32], F32, name="acc", tag="acc", bufs=2)
+            for r, o in enumerate(offsets):
+                for h in range(8):
+                    val = v_rows[g + o // 5][:, wl + o % 5, h, :]
+                    att = es[g][:, 8 * wl + h, o : o + 1]
+                    if r == 0:
+                        nc.vector.tensor_scalar(out=acc[:, 0, h, :], in0=val, scalar1=att, scalar2=None, op0=ALU.mult)
+                    else:
+                        nc.vector.scalar_tensor_tensor(
+                            out=acc[:, 0, h, :], in0=val, scalar=att, in1=acc[:, 0, h, :], op0=ALU.mult, op1=ALU.add
+                        )
+            return acc
+
+        ots = {}
+        done = {}
+
+        def accumulate(late, g, wl, tmp, n_slices, n_offsets):
+            if g not in ots:
+                ots[g] = [psum.tile([P, 512], F32, name="ot%d" % half, tag="w", bufs=2) for half in range(2)]
+            first = done.get((g, wl), 0) == 0
+            done[(g, wl)] = done.get((g, wl), 0) + n_offsets
+            last = done[(g, wl)] == 25
+            for r in range(n_slices):
+                for half in range(2):
+                    nc.tensor.matmul(
+                        out=ots[g][half][:, P * wl : P * (wl + 1)],
+                        lhsT=tmp[:, r, 4 * half : 4 * (half + 1), :].rearrange("p h c -> p (h c)"),
+                        rhs=ident_f[:],
+                        is_transpose=True,
+                        start=(first and r == 0),
+                        stop=(last and r == n_slices - 1),
+                    )
+            if last and wl == 3:
                 for half in range(2):
                     ost = late.tile([P, 16, 8, 4], F32, name="ost", tag="ost", bufs=2)
-                    src = ots[half][:].rearrange("c (wl m wb) -> c m wb wl", wl=4, wb=8)
+                    src = ots[g][half][:].rearrange("c (wl m wb) -> c m wb wl", wl=4, wb=8)
                     if half == 0:
                         nc.vector.tensor_copy(out=ost[:], in_=src)
                     else:
@@ -232,49 +349,98 @@ def tile_relation_kernel(tc, x, w_qkv, out):
                             in_=ost[:, 8 * n : 8 * (n + 1)].rearrange("c m wb wl -> c m (wb wl)"),
                         )
 
-            ssbs = {}
-            late_groups = []
-            for k in range(25):
-                st = psum.tile([P, P], F32, name="st", tag="st", bufs=2)
-                for ch in range(2):
-                    cs = slice(16 * ch, 16 * (ch + 1))
-                    pr = ring.tile([P, 16, 4, 32], F32, name="pr", tag="b8", align_bytes=64)
-                    for s in range(4):
-                        g, o = divmod(4 * k + s, 25)
-                        i, j = divmod(o, 5)
-                        nc.vector.tensor_tensor(
-                            out=pr[:, :, s, :],
-                            in0=q_rows[g][:, cs, :],
-                            in1=k_rows[g + i][:, cs, 8 * j : 8 * j + 32],
-                            op=ALU.mult,
-                        )
-                    for c in range(16):
-                        nc.tensor.matmul(
-                            out=st[:],
-                            lhsT=pr[:, c, :, :].rearrange("p s f -> p (s f)"),
-                            rhs=ident_f[:],
-                            is_transpose=True,
-                            start=(ch == 0 and c == 0),
-                            stop=(ch == 1 and c == 15),
-                        )
-                stsb = soft.tile([P, P], F32, name="stsb", tag="stsb")
-                nc.scalar.copy(out=stsb[:], in_=st[:])
-                sbp = psum.tile([P, 4, 32], F32, name="sbp", tag="sb", bufs=2)
-                nc.tensor.transpose(sbp[:].rearrange("p s f -> p (s f)"), stsb[:], ident_f[:])
-                for g in sorted(set((4 * k + s) // 25 for s in range(4))):
-                    slots = [s for s in range(4) if (4 * k + s) // 25 == g]
-                    o0 = 4 * k + slots[0] - 25 * g
-                    if g not in ssbs:
-                        ssbs[g] = soft.tile([P, 25, 32], F32, name="ssb", tag="ssb")
-                    nc.scalar.copy(
-                        out=ssbs[g][:, o0 : o0 + len(slots), :],
-                        in_=sbp[:, slots[0] : slots[-1] + 1, :],
-                    )
-                    if o0 + len(slots) == 25:
-                        e = softmax(ssbs[g])
-                        if len(VECTOR_PIECES[g]) < 10:
-                            weighted_sum(g, e)
-                        else:
-                            late_groups.append((g, e))
-            for g, e in late_groups:
-                weighted_sum(g, e)
+        state = {"tile": 0, "offset": 0, "made": [], "exp": [], "norm": [], "ready": -1}
+        last_chunk = {(25 * g + 24) // 4: g for g in range(4)}
+
+        def step(late, it):
+            k = it - 2
+            on_tensor = 0 <= k < N_CHUNKS and k not in VECTOR_REDUCED
+            back_due = 0 <= k - 1 < N_CHUNKS and k - 1 not in VECTOR_REDUCED
+            if it + 1 < N_CHUNKS:
+                for g in groups_of(it + 1):
+                    if (g, 0) not in q_banks:
+                        q_bank(g, 0)
+            if 0 <= k < N_CHUNKS and k in VECTOR_REDUCED:
+                vector_reduce(k)
+                if k in last_chunk:
+                    softmax_max(last_chunk[k])
+                    state["exp"].append(last_chunk[k])
+            if it < N_CHUNKS:
+                products(it, 0)
+            for g in state["norm"]:
+                softmax_norm(g)
+                state["ready"] = g
+            state["norm"] = []
+            if it < N_CHUNKS:
+                for g in groups_of(it):
+                    if (g, 1) not in q_banks:
+                        q_bank(g, 1)
+                products(it, 1)
+                fold(it)
+            made = []
+            jobs = []
+            budget = (10 if it < N_CHUNKS else 25) - (5 if state["exp"] else 0)
+            while budget > 0 and state["tile"] < 16 and state["tile"] // 4 <= state["ready"]:
+                g, wl = divmod(state["tile"], 4)
+                o = state["offset"]
+                if o == 0 and it >= N_CHUNKS:
+                    jobs.append((g, wl, None, piece_vector(late, g, wl, list(range(VECTOR_OFFSETS)))))
+                    o = VECTOR_OFFSETS
+                    budget -= VECTOR_OFFSETS
+                n = min(5, 25 - o, budget)
+                jobs.append((g, wl, list(range(o, o + n)), None))
+                budget -= n
+                o += n
+                if o == 25:
+                    state["tile"] += 1
+                    o = 0
+                state["offset"] = o
+            if it < 8:
+                v_row(it)
+            if on_tensor:
+                tensor_reduce(k)
+                warm(WARMERS)
+            if back_due:
+                back(k - 1)
+            for g, wl, tmp, n_slices, n_offsets in state["made"]:
+                accumulate(late, g, wl, tmp, n_slices, n_offsets)
+                warm(WARMERS)
+            copies = [on_tensor, back_due]
+
+            def small_copies():
+                if copies[0]:
+                    copy_st(k)
+                if copies[1]:
+                    copy_back(k - 1)
+                copies[0] = False
+                copies[1] = False
+
+            for g, wl, offsets, acc in jobs:
+                if offsets is None:
+                    made.append((g, wl, acc, 1, VECTOR_OFFSETS))
+                else:
+                    made.append((g, wl, piece_scalar(late, g, wl, offsets), len(offsets), len(offsets)))
+                    small_copies()
+            small_copies()
+            for g in state["exp"]:
+                softmax_exp(late, g)
+                state["norm"].append(g)
+            state["exp"] = []
+            state["made"] = made
+
+        with tc.tile_pool(name="codes", bufs=1) as codes:
+            grps = {}
+            for a in range(9):
+                if a < 8:
+                    grps[a] = gather_row(a)
+                if a >= 1:
+                    quantise_row(codes, a - 1, grps[a - 1])
+                    k_row(a - 1)
+            q_bank(0, 0)
+            for it in range(8):
+                step(None, it)
+        with tc.tile_pool(name="late", bufs=4) as late:
+            it = 8
+            while state["tile"] < 16 or state["made"]:
+                step(late, it)
+                it += 1

@@ -6,6 +6,7 @@ from concourse.masks import make_identity
 F32 = mybir.dt.float32
 BF16 = mybir.dt.bfloat16
 U32 = mybir.dt.uint32
+I32 = mybir.dt.int32
 U8 = mybir.dt.uint8
 FP8X4 = mybir.dt.float8_e4m3fn_x4
 ALU = mybir.AluOpType
@@ -16,9 +17,15 @@ P = 128
 FLOPS = 2 * 768 * 512 * 2048 + 2 * 2 * 2048 * 8 * 25 * 32
 
 N_CHUNKS = 25
-VECTOR_REDUCED = (5, 6, 11, 12, 17, 18, 23, 24)
+GROUPS = ((0, 0, 1), (0, 1, 1), (0, 2, 2), (1, 0, 4), (2, 0, 4), (3, 0, 4))
+VECTOR_REDUCED = (1, 3, 6, 12, 18, 23, 24)
+EVACUATIONS = (("v0", "v1"), ("v2", "v3"), ("v4", "k5"), ("k6", "k7"), ("v5", "v6", "v7"))
 WARMERS = 0
+FOLD_TWICE = ()
 VECTOR_OFFSETS = 13
+VECTOR_MULT = 0
+SCALAR_BUDGET = 10
+TMP_BUFS = 3
 
 
 def tile_relation_kernel(tc, x, w_qkv, out):
@@ -40,6 +47,11 @@ def tile_relation_kernel(tc, x, w_qkv, out):
         v_rows = [keep.tile([P, 8, 8, 32], F32, name="v%d" % r) for r in range(8)]
         core_c = [keep.tile([P, 512], U32, name="cc%d" % r, align_bytes=64) for r in range(4)]
         core_s = [keep.tile([P, 512], U8, name="cs%d" % r, align_bytes=64) for r in range(4)]
+
+        bank_bufs = {"w": 3, "qp": 3, "st": 2}
+
+        def bank(shape, dtype, name, tag):
+            return psum.tile(shape, dtype, name=name, tag=tag, bufs=bank_bufs[tag])
 
         def ring_tile(shape, dtype, name):
             return ring.tile(shape, dtype, name=name, tag="b8", align_bytes=64)
@@ -66,7 +78,7 @@ def tile_relation_kernel(tc, x, w_qkv, out):
         wgrp = ring_tile([P, 768, 4], BF16, "wgrp")
         for r in range(6):
             ty, hh = divmod(r, 2)
-            wt = psum.tile([P, 4, P], BF16, name="wt", tag="w", bufs=2)
+            wt = bank([P, 4, P], BF16, "wt", "w")
             for t in range(4):
                 nc.tensor.transpose(wt[:, t, :], wraw[:, r, P * t : P * (t + 1)], ident_b[:])
             if ty < 2:
@@ -105,20 +117,13 @@ def tile_relation_kernel(tc, x, w_qkv, out):
                     )
 
         tiles = {}
+        row_parts = {}
 
         def gather_row(a):
             grp = ring_tile([P, 4096], BF16, "grp")
             g_f = grp[:].bitcast(F32).rearrange("p (b n hb wb u) -> p b n hb wb u", b=8, n=2, hb=8, wb=8)
             nc.vector.memset(g_f[:, 0:2, :, :, 0, :], 0.0)
             nc.vector.memset(g_f[:, 6:8, :, :, 7, :], 0.0)
-            if a < 2:
-                nc.vector.memset(g_f[:, :, :, 0, :, :], 0.0)
-                hl_src, hd, hs = a + 2, slice(1, 8), slice(0, 7)
-            elif a < 6:
-                hl_src, hd, hs = a - 2, slice(0, 8), slice(0, 8)
-            else:
-                nc.vector.memset(g_f[:, :, :, 7, :, :], 0.0)
-                hl_src, hd, hs = a - 6, slice(0, 7), slice(1, 8)
             for n in range(2):
                 for bs, wls, wd, wsrc in (
                     (slice(0, 2), slice(2, 4), slice(1, 8), slice(0, 7)),
@@ -126,101 +131,149 @@ def tile_relation_kernel(tc, x, w_qkv, out):
                     (slice(6, 8), slice(0, 2), slice(0, 7), slice(1, 8)),
                 ):
                     nc.vector.tensor_copy(
-                        out=g_f[:, bs, n, hd, wd, :],
-                        in_=inters[n][:, hs, hl_src, wsrc, wls, :].rearrange("p hb wb wl u -> p wl hb wb u"),
+                        out=g_f[:, bs, n, :, wd, :],
+                        in_=inters[n][:, :, a - 2, wsrc, wls, :].rearrange("p hb wb wl u -> p wl hb wb u"),
                     )
             return grp
 
+        def name_tiles(a, parts):
+            row_parts[a] = parts
+            for b0, b1, c_ap, s_ap in parts:
+                for b in range(b0, b1):
+                    cols = slice(P * (b - b0), P * (b - b0 + 1))
+                    tiles[(a, b)] = (c_ap[:, cols], s_ap[:, cols])
+
         def quantise_row(codes, a, grp):
-            if 2 <= a < 6:
-                hc = codes.tile([P, 512], U32, name="hc%d" % a, align_bytes=64)
-                hs_ = codes.tile([P, 512], U8, name="hs%d" % a, align_bytes=64)
-                parts = (
-                    (0, 2, hc[:, 0:256], hs_[:, 0:256]),
-                    (2, 6, core_c[a - 2][:], core_s[a - 2][:]),
-                    (6, 8, hc[:, 256:512], hs_[:, 256:512]),
-                )
-            else:
-                hc = codes.tile([P, 1024], U32, name="hc%d" % a, align_bytes=64)
-                hs_ = codes.tile([P, 1024], U8, name="hs%d" % a, align_bytes=64)
-                parts = ((0, 8, hc[:], hs_[:]),)
+            hc = codes.tile([P, 512], U32, name="hc%d" % a, align_bytes=64)
+            hs = codes.tile([P, 512], U8, name="hs%d" % a, align_bytes=64)
+            parts = (
+                (0, 2, hc[:, 0:256], hs[:, 0:256]),
+                (2, 6, core_c[a - 2][:], core_s[a - 2][:]),
+                (6, 8, hc[:, 256:512], hs[:, 256:512]),
+            )
             for b0, b1, c_ap, s_ap in parts:
                 nc.vector.quantize_mx(out=c_ap.bitcast(FP8X4), scales=s_ap, in_=grp[:, 512 * b0 : 512 * b1])
-                for b in range(b0, b1):
-                    tiles[(a, b)] = (c_ap[:, P * (b - b0) : P * (b - b0 + 1)], s_ap[:, P * (b - b0) : P * (b - b0 + 1)])
+            name_tiles(a, parts)
 
-        def k_row(a):
-            for b0 in (0, 2, 4, 6):
-                ps = psum.tile([P, 2, 256], F32, name="ps", tag="w", bufs=2)
-                for u in range(2):
-                    project(ps[:, u, :], tiles[(a, b0 + u)][0], tiles[(a, b0 + u)][1], 256, 512)
-                nc.scalar.copy(
-                    out=k_rows[a][:, :, 8 * b0 : 8 * (b0 + 2)].rearrange("p c (u h) -> p c u h", h=8),
-                    in_=ps[:].rearrange("p u (c h) -> p c u h", h=8),
-                )
+        def move_row(codes, a):
+            hc = codes.tile([P, 1024], U32, name="hc%d" % a, align_bytes=64)
+            hs = codes.tile([P, 1024], U8, name="hs%d" % a, align_bytes=64)
+            for which, dst_t, width, sh in ((2, hc, 64, 8), (3, hs, 16, 2)):
+                dst = dst_t[:].bitcast(I32).rearrange("p (m x) -> p m x", x=width)
+                nc.vector.memset(dst[:, :, 0:sh] if a < 2 else dst[:, :, width - sh : width], 0)
+                for part in row_parts[a + 4 if a < 2 else a - 4]:
+                    src = part[which].bitcast(I32).rearrange("p (m x) -> p m x", x=width)
+                    rows = slice(2 * part[0], 2 * part[1])
+                    if a < 2:
+                        nc.vector.tensor_copy(out=dst[:, rows, sh:width], in_=src[:, :, 0 : width - sh])
+                    else:
+                        nc.vector.tensor_copy(out=dst[:, rows, 0 : width - sh], in_=src[:, :, sh:width])
+            name_tiles(a, ((0, 8, hc[:], hs[:]),))
 
-        def v_row(a):
-            for b0 in (0, 2, 4, 6):
-                ps = psum.tile([P, 2, 256], F32, name="ps", tag="w", bufs=2)
+        def evacuate(what, a, tags):
+            for r, b0 in enumerate((0, 2, 4, 6)):
+                ps = bank([P, 2, 256], F32, "ps", tags[r % len(tags)])
                 for u in range(2):
-                    project(ps[:, u, :], tiles[(a, b0 + u)][0], tiles[(a, b0 + u)][1], 512, 768)
-                nc.scalar.copy(out=v_rows[a][:, b0 : b0 + 2, :, :].rearrange("p b h c -> p b (h c)"), in_=ps[:])
+                    lo = 256 if what == "k" else 512
+                    project(ps[:, u, :], tiles[(a, b0 + u)][0], tiles[(a, b0 + u)][1], lo, lo + 256)
+                if what == "k":
+                    nc.scalar.copy(
+                        out=k_rows[a][:, :, 8 * b0 : 8 * (b0 + 2)].rearrange("p c (u h) -> p c u h", h=8),
+                        in_=ps[:].rearrange("p u (c h) -> p c u h", h=8),
+                    )
+                else:
+                    nc.scalar.copy(out=v_rows[a][:, b0 : b0 + 2, :, :].rearrange("p b h c -> p b (h c)"), in_=ps[:])
+
+        chunks = [[] for k in range(N_CHUNKS)]
+        col = 0
+        for gi, (hl, wl0, nt) in enumerate(GROUPS):
+            for o in range(25):
+                chunks[col // P].append((gi, o, col % P))
+                col += 8 * nt
+        max_step = {}
+        for k in range(N_CHUNKS):
+            for gi, o, f0 in chunks[k]:
+                max_step[gi] = max(max_step.get(gi, 0), k + 2 if k in VECTOR_REDUCED else k + 4)
+        group_of_tile = {}
+        for gi, (hl, wl0, nt) in enumerate(GROUPS):
+            for wl in range(wl0, wl0 + nt):
+                group_of_tile[4 * hl + wl] = gi
 
         q_banks = {}
 
-        def q_bank(g, ch):
-            qp = psum.tile([P, 4, 16, 8], F32, name="qp", tag="qp", bufs=3)
+        def q_bank(hl, ch):
+            qp = bank([P, 4, 16, 8], F32, "qp", "qp")
             for wl in range(4):
                 project(
                     qp[:, wl, :, :].rearrange("p c h -> p (c h)"),
-                    tiles[(g + 2, wl + 2)][0],
-                    tiles[(g + 2, wl + 2)][1],
+                    tiles[(hl + 2, wl + 2)][0],
+                    tiles[(hl + 2, wl + 2)][1],
                     P * ch,
                     P * (ch + 1),
                 )
-            q_banks[(g, ch)] = qp
+            q_banks[(hl, ch)] = qp
 
-        def groups_of(k):
-            return sorted(set((4 * k + s) // 25 for s in range(4)))
+        def rows_of(k):
+            return sorted(set(GROUPS[gi][0] for gi, o, f0 in chunks[k]))
 
         halves = {}
 
         def products(k, ch):
             cs = slice(16 * ch, 16 * (ch + 1))
-            pr = ring_tile([P, 16, 4, 32], F32, "pr")
-            for s in range(4):
-                g, o = divmod(4 * k + s, 25)
+            pr = ring_tile([P, 16, P], F32, "pr")
+            todo = list(chunks[k])
+            while todo:
+                gi, o, f0 = todo[0]
+                hl, wl0, nt = GROUPS[gi]
                 i, j = divmod(o, 5)
+                run = 1
+                if nt == 1:
+                    while run < len(todo) and run < 5 - j and todo[run][0] == gi:
+                        run += 1
+                todo = todo[run:]
+                w = 8 * nt * run
+                qv = q_banks[(hl, ch)][:, wl0 : wl0 + nt, :, :].rearrange("p wl c h -> p c wl h")
+                if run > 1:
+                    qv = qv.to_broadcast([P, 16, run, 8])
                 nc.vector.tensor_tensor(
-                    out=pr[:, :, s, :].rearrange("p c (wl h) -> p c wl h", h=8),
-                    in0=q_banks[(g, ch)][:].rearrange("p wl c h -> p c wl h"),
-                    in1=k_rows[g + i][:, cs, 8 * j : 8 * j + 32].rearrange("p c (wl h) -> p c wl h", h=8),
+                    out=pr[:, :, f0 : f0 + w].rearrange("p c (wl h) -> p c wl h", h=8),
+                    in0=qv,
+                    in1=k_rows[hl + i][:, cs, 8 * (wl0 + j) : 8 * (wl0 + j) + w].rearrange("p c (wl h) -> p c wl h", h=8),
                     op=ALU.mult,
                 )
             halves[(k, ch)] = pr
 
         def fold(k):
-            a_ap = halves[(k, 0)][:].rearrange("p c s f -> p (c s f)")
-            nc.gpsimd.tensor_tensor(
-                out=a_ap, in0=a_ap, in1=halves[(k, 1)][:].rearrange("p c s f -> p (c s f)"), op=ALU.add
-            )
+            a_ap = halves[(k, 0)][:].rearrange("p c f -> p (c f)")
+            nc.gpsimd.tensor_tensor(out=a_ap, in0=a_ap, in1=halves[(k, 1)][:].rearrange("p c f -> p (c f)"), op=ALU.add)
+            if k in FOLD_TWICE:
+                nc.gpsimd.tensor_tensor(out=a_ap[:, 0:1024], in0=a_ap[:, 0:1024], in1=a_ap[:, 1024:2048], op=ALU.add)
+
+        def left(k):
+            return 8 if k in FOLD_TWICE else 16
 
         ssbs = {}
 
         def score_parts(k):
             parts = []
-            for g in groups_of(k):
-                slots = [s for s in range(4) if (4 * k + s) // 25 == g]
-                if g not in ssbs:
-                    ssbs[g] = soft.tile([P, 25, 32], F32, name="ssb", tag="ssb")
-                o0 = 4 * k + slots[0] - 25 * g
-                parts.append((ssbs[g][:, o0 : o0 + len(slots), :], slots[0], slots[-1] + 1))
+            for gi in sorted(set(s[0] for s in chunks[k])):
+                mine = [s for s in chunks[k] if s[0] == gi]
+                w = 8 * GROUPS[gi][2]
+                if gi not in ssbs:
+                    if w < 32:
+                        ssbs[gi] = soft.tile([P, 25, w], F32, name="ssn", tag="ssn", bufs=3)
+                    else:
+                        ssbs[gi] = soft.tile([P, 25, w], F32, name="ssb", tag="ssb")
+                parts.append((ssbs[gi][:, mine[0][1] : mine[-1][1] + 1, :], mine[0][2], mine[-1][2] + w, w))
             return parts
 
         def vector_reduce(k):
-            for dst, s0, s1 in score_parts(k):
+            for dst, f0, f1, w in score_parts(k):
                 nc.vector.tensor_reduce(
-                    out=dst, in_=halves[(k, 0)][:, :, s0:s1, :].rearrange("p c s f -> p s f c"), axis=AX.X, op=ALU.add
+                    out=dst,
+                    in_=halves[(k, 0)][:, 0 : left(k), f0:f1].rearrange("p c (s f) -> p s f c", f=w),
+                    axis=AX.X,
+                    op=ALU.add,
                 )
 
         sts = {}
@@ -231,15 +284,15 @@ def tile_relation_kernel(tc, x, w_qkv, out):
                 project(dm[:], wc[:, 0:P], ws[:, 0:P], 256, 768)
 
         def tensor_reduce(k):
-            st = psum.tile([P, P], F32, name="st", tag="st", bufs=2)
-            for c in range(16):
+            st = bank([P, P], F32, "st", "st")
+            for c in range(left(k)):
                 nc.tensor.matmul(
                     out=st[:],
-                    lhsT=halves[(k, 0)][:, c, :, :].rearrange("p s f -> p (s f)"),
+                    lhsT=halves[(k, 0)][:, c, :],
                     rhs=ident_f[:],
                     is_transpose=True,
                     start=(c == 0),
-                    stop=(c == 15),
+                    stop=(c == left(k) - 1),
                 )
             sts[k] = st
 
@@ -249,79 +302,111 @@ def tile_relation_kernel(tc, x, w_qkv, out):
             sts[k] = stsb
 
         def back(k):
-            sbp = psum.tile([P, 4, 32], F32, name="sbp", tag="st", bufs=2)
-            nc.tensor.transpose(sbp[:].rearrange("p s f -> p (s f)"), sts[k][:], ident_f[:])
+            sbp = bank([P, P], F32, "sbp", "st")
+            nc.tensor.transpose(sbp[:], sts[k][:], ident_f[:])
             sts[k] = sbp
 
         def copy_back(k):
-            for dst, s0, s1 in score_parts(k):
-                nc.scalar.copy(out=dst, in_=sts[k][:, s0:s1, :])
+            for dst, f0, f1, w in score_parts(k):
+                nc.scalar.copy(out=dst, in_=sts[k][:, f0:f1].rearrange("p (s f) -> p s f", f=w))
 
         nmxs = {}
         es = {}
         sums = {}
 
-        def softmax_max(g):
-            mx = soft.tile([P, 32], F32, name="mx", tag="mx")
-            nc.vector.tensor_reduce(out=mx[:], in_=ssbs[g][:].rearrange("p o f -> p f o"), axis=AX.X, op=ALU.max)
-            nmx = soft.tile([P, 32], F32, name="nmx", tag="nmx")
+        def softmax_max(gi):
+            w = 8 * GROUPS[gi][2]
+            mx = soft.tile([P, w], F32, name="mx", tag="mx")
+            nc.vector.tensor_reduce(out=mx[:], in_=ssbs[gi][:].rearrange("p o f -> p f o"), axis=AX.X, op=ALU.max)
+            nmx = soft.tile([P, w], F32, name="nmx", tag="nmx")
             nc.vector.tensor_scalar(out=nmx[:], in0=mx[:], scalar1=-1.0, scalar2=None, op0=ALU.mult)
-            nmxs[g] = nmx
+            nmxs[gi] = nmx
 
-        def softmax_exp(late, g):
-            e = late.tile([P, 32, 25], F32, name="e", tag="e", bufs=3)
-            ssum = soft.tile([P, 32], F32, name="ssum", tag="ssum")
-            for f in range(32):
+        def softmax_exp(late, gi):
+            w = 8 * GROUPS[gi][2]
+            if w < 32:
+                e = soft.tile([P, w, 25], F32, name="en", tag="en", bufs=3)
+            else:
+                e = late.tile([P, w, 25], F32, name="e", tag="e", bufs=3)
+            ssum = soft.tile([P, w], F32, name="ssum", tag="ssum")
+            for f in range(w):
                 nc.scalar.activation(
                     out=e[:, f, :],
-                    in_=ssbs[g][:, :, f],
+                    in_=ssbs[gi][:, :, f],
                     func=ACT.Exp,
-                    bias=nmxs[g][:, f : f + 1],
+                    bias=nmxs[gi][:, f : f + 1],
                     scale=1.0,
                     accum_out=ssum[:, f : f + 1],
                 )
-            es[g] = e
-            sums[g] = ssum
+            es[gi] = e
+            sums[gi] = ssum
 
-        def softmax_norm(g):
-            rs = soft.tile([P, 32], F32, name="rs", tag="rs")
-            nc.vector.reciprocal(out=rs[:], in_=sums[g][:])
+        def softmax_norm(gi):
+            w = 8 * GROUPS[gi][2]
+            rs = soft.tile([P, w], F32, name="rs", tag="rs")
+            nc.vector.reciprocal(out=rs[:], in_=sums[gi][:])
             nc.vector.tensor_tensor(
-                out=es[g][:], in0=es[g][:], in1=rs[:].unsqueeze(2).to_broadcast([P, 32, 25]), op=ALU.mult
+                out=es[gi][:], in0=es[gi][:], in1=rs[:].unsqueeze(2).to_broadcast([P, w, 25]), op=ALU.mult
             )
 
-        def piece_scalar(late, g, wl, offsets):
-            tmp = late.tile([P, 5, 8, 32], F32, name="tmp", tag="tmp", bufs=4)
+        def weights(hl, wl):
+            gi = group_of_tile[4 * hl + wl]
+            f0 = 8 * (wl - GROUPS[gi][1])
+            return es[gi][:, f0 : f0 + 8, :]
+
+        def piece_scalar(late, hl, wl, offsets):
+            tmp = late.tile([P, 5, 8, 32], F32, name="tmp", tag="tmp", bufs=TMP_BUFS)
+            att = weights(hl, wl)
             for r, o in enumerate(offsets):
                 for h in range(8):
                     nc.scalar.activation(
                         out=tmp[:, r, h, :],
-                        in_=v_rows[g + o // 5][:, wl + o % 5, h, :],
+                        in_=v_rows[hl + o // 5][:, wl + o % 5, h, :],
                         func=ACT.Copy,
-                        scale=es[g][:, 8 * wl + h, o : o + 1],
+                        scale=att[:, h, o : o + 1],
                     )
             return tmp
 
-        def piece_vector(late, g, wl, offsets):
+        def piece_fused(late, hl, wl, offsets):
             acc = late.tile([P, 1, 8, 32], F32, name="acc", tag="acc", bufs=2)
+            att = weights(hl, wl)
             for r, o in enumerate(offsets):
                 for h in range(8):
-                    val = v_rows[g + o // 5][:, wl + o % 5, h, :]
-                    att = es[g][:, 8 * wl + h, o : o + 1]
+                    val = v_rows[hl + o // 5][:, wl + o % 5, h, :]
                     if r == 0:
-                        nc.vector.tensor_scalar(out=acc[:, 0, h, :], in0=val, scalar1=att, scalar2=None, op0=ALU.mult)
+                        nc.vector.tensor_scalar(
+                            out=acc[:, 0, h, :], in0=val, scalar1=att[:, h, o : o + 1], scalar2=None, op0=ALU.mult
+                        )
                     else:
                         nc.vector.scalar_tensor_tensor(
-                            out=acc[:, 0, h, :], in0=val, scalar=att, in1=acc[:, 0, h, :], op0=ALU.mult, op1=ALU.add
+                            out=acc[:, 0, h, :],
+                            in0=val,
+                            scalar=att[:, h, o : o + 1],
+                            in1=acc[:, 0, h, :],
+                            op0=ALU.mult,
+                            op1=ALU.add,
                         )
             return acc
+
+        def piece_mult(late, hl, wl, i):
+            tmp = late.tile([P, 5, 8, 32], F32, name="tmp", tag="tmp", bufs=TMP_BUFS)
+            nc.vector.tensor_tensor(
+                out=tmp[:],
+                in0=v_rows[hl + i][:, wl : wl + 5, :, :],
+                in1=weights(hl, wl)[:, :, 5 * i : 5 * (i + 1)]
+                .rearrange("p h j -> p j h")
+                .unsqueeze(3)
+                .to_broadcast([P, 5, 8, 32]),
+                op=ALU.mult,
+            )
+            return tmp
 
         ots = {}
         done = {}
 
         def accumulate(late, g, wl, tmp, n_slices, n_offsets):
             if g not in ots:
-                ots[g] = [psum.tile([P, 512], F32, name="ot%d" % half, tag="w", bufs=2) for half in range(2)]
+                ots[g] = [bank([P, 512], F32, "ot%d" % half, "w") for half in range(2)]
             first = done.get((g, wl), 0) == 0
             done[(g, wl)] = done.get((g, wl), 0) + n_offsets
             last = done[(g, wl)] == 25
@@ -350,53 +435,62 @@ def tile_relation_kernel(tc, x, w_qkv, out):
                         )
 
         state = {"tile": 0, "offset": 0, "made": [], "exp": [], "norm": [], "ready": -1}
-        last_chunk = {(25 * g + 24) // 4: g for g in range(4)}
 
         def step(late, it):
             k = it - 2
             on_tensor = 0 <= k < N_CHUNKS and k not in VECTOR_REDUCED
             back_due = 0 <= k - 1 < N_CHUNKS and k - 1 not in VECTOR_REDUCED
             if it + 1 < N_CHUNKS:
-                for g in groups_of(it + 1):
-                    if (g, 0) not in q_banks:
-                        q_bank(g, 0)
+                for hl in rows_of(it + 1):
+                    if (hl, 0) not in q_banks:
+                        q_bank(hl, 0)
             if 0 <= k < N_CHUNKS and k in VECTOR_REDUCED:
                 vector_reduce(k)
-                if k in last_chunk:
-                    softmax_max(last_chunk[k])
-                    state["exp"].append(last_chunk[k])
+            for gi in range(len(GROUPS)):
+                if max_step[gi] == it:
+                    softmax_max(gi)
+                    state["exp"].append(gi)
             if it < N_CHUNKS:
                 products(it, 0)
-            for g in state["norm"]:
-                softmax_norm(g)
-                state["ready"] = g
+            for gi in state["norm"]:
+                softmax_norm(gi)
+                state["ready"] = gi
             state["norm"] = []
             if it < N_CHUNKS:
-                for g in groups_of(it):
-                    if (g, 1) not in q_banks:
-                        q_bank(g, 1)
+                for hl in rows_of(it):
+                    if (hl, 1) not in q_banks:
+                        q_bank(hl, 1)
                 products(it, 1)
                 fold(it)
             made = []
             jobs = []
-            budget = (10 if it < N_CHUNKS else 25) - (5 if state["exp"] else 0)
-            while budget > 0 and state["tile"] < 16 and state["tile"] // 4 <= state["ready"]:
+            budget = SCALAR_BUDGET - (5 if state["exp"] else 0)
+            while late is not None and budget > 0 and state["tile"] < 16 and group_of_tile[state["tile"]] <= state["ready"]:
                 g, wl = divmod(state["tile"], 4)
                 o = state["offset"]
-                if o == 0 and it >= N_CHUNKS:
-                    jobs.append((g, wl, None, piece_vector(late, g, wl, list(range(VECTOR_OFFSETS)))))
-                    o = VECTOR_OFFSETS
-                    budget -= VECTOR_OFFSETS
+                if it >= N_CHUNKS:
+                    if VECTOR_MULT and o == 0:
+                        jobs.append((g, wl, "mult", None, 5, 5))
+                        o = 5
+                    n = ((25 - o) * VECTOR_OFFSETS + 12) // 25
+                    jobs.append((g, wl, None, piece_fused(late, g, wl, list(range(o, o + n))), 1, n))
+                    o += n
+                    budget = 25 - o
                 n = min(5, 25 - o, budget)
-                jobs.append((g, wl, list(range(o, o + n)), None))
-                budget -= n
-                o += n
+                while n > 0:
+                    jobs.append((g, wl, list(range(o, o + n)), None, n, n))
+                    budget -= n
+                    o += n
+                    n = min(5, 25 - o, budget)
                 if o == 25:
                     state["tile"] += 1
                     o = 0
                 state["offset"] = o
-            if it < 8:
-                v_row(it)
+                if it >= N_CHUNKS:
+                    budget = 0
+            if it < len(EVACUATIONS):
+                for name in EVACUATIONS[it]:
+                    evacuate(name[0], int(name[1]), ("w",))
             if on_tensor:
                 tensor_reduce(k)
                 warm(WARMERS)
@@ -415,32 +509,45 @@ def tile_relation_kernel(tc, x, w_qkv, out):
                 copies[0] = False
                 copies[1] = False
 
-            for g, wl, offsets, acc in jobs:
+            for g, wl, offsets, tmp, n_slices, n_offsets in jobs:
                 if offsets is None:
-                    made.append((g, wl, acc, 1, VECTOR_OFFSETS))
+                    made.append((g, wl, tmp, n_slices, n_offsets))
+                elif offsets == "mult":
+                    made.append((g, wl, piece_mult(late, g, wl, 0), n_slices, n_offsets))
                 else:
-                    made.append((g, wl, piece_scalar(late, g, wl, offsets), len(offsets), len(offsets)))
+                    made.append((g, wl, piece_scalar(late, g, wl, offsets), n_slices, n_offsets))
                     small_copies()
             small_copies()
-            for g in state["exp"]:
-                softmax_exp(late, g)
-                state["norm"].append(g)
+            for gi in state["exp"]:
+                softmax_exp(late, gi)
+                state["norm"].append(gi)
             state["exp"] = []
             state["made"] = made
 
         with tc.tile_pool(name="codes", bufs=1) as codes:
-            grps = {}
-            for a in range(9):
-                if a < 8:
-                    grps[a] = gather_row(a)
-                if a >= 1:
-                    quantise_row(codes, a - 1, grps[a - 1])
-                    k_row(a - 1)
+            every = ("w", "qp", "st")
+            g2 = gather_row(2)
+            g4 = gather_row(4)
+            quantise_row(codes, 2, g2)
+            evacuate("k", 2, every)
+            g5 = gather_row(5)
+            quantise_row(codes, 4, g4)
+            move_row(codes, 0)
+            evacuate("k", 0, every)
+            g3 = gather_row(3)
+            quantise_row(codes, 5, g5)
+            move_row(codes, 1)
+            evacuate("k", 1, every)
+            quantise_row(codes, 3, g3)
+            evacuate("k", 3, every)
+            evacuate("k", 4, every)
             q_bank(0, 0)
-            for it in range(8):
+            move_row(codes, 6)
+            move_row(codes, 7)
+            for it in range(len(EVACUATIONS)):
                 step(None, it)
         with tc.tile_pool(name="late", bufs=4) as late:
-            it = 8
+            it = len(EVACUATIONS)
             while state["tile"] < 16 or state["made"]:
                 step(late, it)
                 it += 1

@@ -26,6 +26,9 @@ VECTOR_OFFSETS = 13
 VECTOR_MULT = 0
 SCALAR_BUDGET = 10
 TMP_BUFS = 3
+FOLD_EVERY = 2
+K_DEAD_LAG = 0
+K_ROWS_REUSED = 2
 
 
 def tile_relation_kernel(tc, x, w_qkv, out):
@@ -194,6 +197,10 @@ def tile_relation_kernel(tc, x, w_qkv, out):
         for k in range(N_CHUNKS):
             for gi, o, f0 in chunks[k]:
                 max_step[gi] = max(max_step.get(gi, 0), k + 2 if k in VECTOR_REDUCED else k + 4)
+        K_DEAD = {}
+        for k in range(N_CHUNKS):
+            for gi, o, f0 in chunks[k]:
+                K_DEAD[GROUPS[gi][0] + o // 5] = k + K_DEAD_LAG
         group_of_tile = {}
         for gi, (hl, wl0, nt) in enumerate(GROUPS):
             for wl in range(wl0, wl0 + nt):
@@ -354,8 +361,23 @@ def tile_relation_kernel(tc, x, w_qkv, out):
             f0 = 8 * (wl - GROUPS[gi][1])
             return es[gi][:, f0 : f0 + 8, :]
 
-        def piece_scalar(late, hl, wl, offsets):
-            tmp = late.tile([P, 5, 8, 32], F32, name="tmp", tag="tmp", bufs=TMP_BUFS)
+        free_tags = ["tmp"] * TMP_BUFS
+        freed_rows = []
+
+        def tmp_tile(late, it):
+            for a in range(8):
+                if it > K_DEAD[a] and a not in freed_rows and len(freed_rows) < K_ROWS_REUSED:
+                    freed_rows.append(a)
+                    free_tags.append("k%d" % a)
+            tag = free_tags.pop(0)
+            if tag == "tmp":
+                tmp = late.tile([P, 5, 8, 32], F32, name="tmp", tag="tmp", bufs=TMP_BUFS)
+            else:
+                tmp = keep.tile([P, 5, 8, 32], F32, name="tmk", tag=tag)
+            return tmp, tag
+
+        def piece_scalar(late, hl, wl, offsets, it):
+            tmp, tag = tmp_tile(late, it)
             att = weights(hl, wl)
             for r, o in enumerate(offsets):
                 for h in range(8):
@@ -365,7 +387,7 @@ def tile_relation_kernel(tc, x, w_qkv, out):
                         func=ACT.Copy,
                         scale=att[:, h, o : o + 1],
                     )
-            return tmp
+            return tmp, tag
 
         def piece_fused(late, hl, wl, offsets):
             acc = late.tile([P, 1, 8, 32], F32, name="acc", tag="acc", bufs=2)
@@ -388,8 +410,8 @@ def tile_relation_kernel(tc, x, w_qkv, out):
                         )
             return acc
 
-        def piece_mult(late, hl, wl, i):
-            tmp = late.tile([P, 5, 8, 32], F32, name="tmp", tag="tmp", bufs=TMP_BUFS)
+        def piece_mult(late, hl, wl, i, it):
+            tmp, tag = tmp_tile(late, it)
             nc.vector.tensor_tensor(
                 out=tmp[:],
                 in0=v_rows[hl + i][:, wl : wl + 5, :, :],
@@ -399,7 +421,7 @@ def tile_relation_kernel(tc, x, w_qkv, out):
                 .to_broadcast([P, 5, 8, 32]),
                 op=ALU.mult,
             )
-            return tmp
+            return tmp, tag
 
         ots = {}
         done = {}
@@ -434,12 +456,19 @@ def tile_relation_kernel(tc, x, w_qkv, out):
                             in_=ost[:, 8 * n : 8 * (n + 1)].rearrange("c m wb wl -> c m (wb wl)"),
                         )
 
-        state = {"tile": 0, "offset": 0, "made": [], "exp": [], "norm": [], "ready": -1}
+        state = {"tile": 0, "offset": 0, "made": [], "exp": [], "norm": [], "ready": -1, "fold": [], "folded": []}
 
         def step(late, it):
             k = it - 2
             on_tensor = 0 <= k < N_CHUNKS and k not in VECTOR_REDUCED
             back_due = 0 <= k - 1 < N_CHUNKS and k - 1 not in VECTOR_REDUCED
+            folded = []
+            for g, wl, t0, t1 in state["fold"]:
+                a_ap = t0[0][:].rearrange("p j h c -> p (j h c)")
+                nc.gpsimd.tensor_tensor(out=a_ap, in0=a_ap, in1=t1[0][:].rearrange("p j h c -> p (j h c)"), op=ALU.add)
+                free_tags.append(t1[1])
+                folded.append((g, wl, t0, 5, 10))
+            state["fold"] = []
             if it + 1 < N_CHUNKS:
                 for hl in rows_of(it + 1):
                     if (hl, 0) not in q_banks:
@@ -473,7 +502,7 @@ def tile_relation_kernel(tc, x, w_qkv, out):
                         jobs.append((g, wl, "mult", None, 5, 5))
                         o = 5
                     n = ((25 - o) * VECTOR_OFFSETS + 12) // 25
-                    jobs.append((g, wl, None, piece_fused(late, g, wl, list(range(o, o + n))), 1, n))
+                    fused = (g, wl, None, (piece_fused(late, g, wl, list(range(o, o + n))), None), 1, n)
                     o += n
                     budget = 25 - o
                 n = min(5, 25 - o, budget)
@@ -482,6 +511,8 @@ def tile_relation_kernel(tc, x, w_qkv, out):
                     budget -= n
                     o += n
                     n = min(5, 25 - o, budget)
+                if it >= N_CHUNKS:
+                    jobs.append(fused)
                 if o == 25:
                     state["tile"] += 1
                     o = 0
@@ -496,9 +527,12 @@ def tile_relation_kernel(tc, x, w_qkv, out):
                 warm(WARMERS)
             if back_due:
                 back(k - 1)
-            for g, wl, tmp, n_slices, n_offsets in state["made"]:
-                accumulate(late, g, wl, tmp, n_slices, n_offsets)
+            for g, wl, tmp, n_slices, n_offsets in state["folded"] + state["made"]:
+                accumulate(late, g, wl, tmp[0], n_slices, n_offsets)
+                if tmp[1] is not None:
+                    free_tags.append(tmp[1])
                 warm(WARMERS)
+            state["folded"] = folded
             copies = [on_tensor, back_due]
 
             def small_copies():
@@ -513,15 +547,25 @@ def tile_relation_kernel(tc, x, w_qkv, out):
                 if offsets is None:
                     made.append((g, wl, tmp, n_slices, n_offsets))
                 elif offsets == "mult":
-                    made.append((g, wl, piece_mult(late, g, wl, 0), n_slices, n_offsets))
+                    made.append((g, wl, piece_mult(late, g, wl, 0, it), n_slices, n_offsets))
                 else:
-                    made.append((g, wl, piece_scalar(late, g, wl, offsets), n_slices, n_offsets))
+                    made.append((g, wl, piece_scalar(late, g, wl, offsets, it), n_slices, n_offsets))
                     small_copies()
             small_copies()
             for gi in state["exp"]:
                 softmax_exp(late, gi)
                 state["norm"].append(gi)
             state["exp"] = []
+            if (
+                it < N_CHUNKS
+                and it % FOLD_EVERY == 0
+                and len(made) == 2
+                and made[0][:2] == made[1][:2]
+                and made[0][3] == 5
+                and made[1][3] == 5
+            ):
+                state["fold"].append((made[0][0], made[0][1], made[0][2], made[1][2]))
+                made = []
             state["made"] = made
 
         with tc.tile_pool(name="codes", bufs=1) as codes:
@@ -548,6 +592,6 @@ def tile_relation_kernel(tc, x, w_qkv, out):
                 step(None, it)
         with tc.tile_pool(name="late", bufs=4) as late:
             it = len(EVACUATIONS)
-            while state["tile"] < 16 or state["made"]:
+            while state["tile"] < 16 or state["made"] or state["fold"] or state["folded"]:
                 step(late, it)
                 it += 1

@@ -26,7 +26,8 @@ VECTOR_OFFSETS = 13
 VECTOR_MULT = 0
 SCALAR_BUDGET = 10
 TMP_BUFS = 3
-FOLD_EVERY = 2
+FOLD_EVERY = 99
+EARLY_OFFSETS = 0
 K_DEAD_LAG = 0
 K_ROWS_REUSED = 2
 
@@ -456,7 +457,7 @@ def tile_relation_kernel(tc, x, w_qkv, out):
                             in_=ost[:, 8 * n : 8 * (n + 1)].rearrange("c m wb wl -> c m (wb wl)"),
                         )
 
-        state = {"tile": 0, "offset": 0, "made": [], "exp": [], "norm": [], "ready": -1, "fold": [], "folded": []}
+        state = {"tile": 0, "offset": 0, "made": [], "exp": [], "norm": [], "ready": -1, "fold": [], "folded": [], "fused": None}
 
         def step(late, it):
             k = it - 2
@@ -497,13 +498,12 @@ def tile_relation_kernel(tc, x, w_qkv, out):
             while late is not None and budget > 0 and state["tile"] < 16 and group_of_tile[state["tile"]] <= state["ready"]:
                 g, wl = divmod(state["tile"], 4)
                 o = state["offset"]
-                if it >= N_CHUNKS:
-                    if VECTOR_MULT and o == 0:
-                        jobs.append((g, wl, "mult", None, 5, 5))
-                        o = 5
-                    n = ((25 - o) * VECTOR_OFFSETS + 12) // 25
-                    fused = (g, wl, None, (piece_fused(late, g, wl, list(range(o, o + n))), None), 1, n)
+                share = VECTOR_OFFSETS if it >= N_CHUNKS else EARLY_OFFSETS
+                if share and (o == 0 or (it >= N_CHUNKS and state["fused"] is None)):
+                    n = ((25 - o) * share + 12) // 25
+                    state["fused"] = (g, wl, None, (piece_fused(late, g, wl, list(range(o, o + n))), None), 1, n)
                     o += n
+                if it >= N_CHUNKS:
                     budget = 25 - o
                 n = min(5, 25 - o, budget)
                 while n > 0:
@@ -511,9 +511,10 @@ def tile_relation_kernel(tc, x, w_qkv, out):
                     budget -= n
                     o += n
                     n = min(5, 25 - o, budget)
-                if it >= N_CHUNKS:
-                    jobs.append(fused)
                 if o == 25:
+                    if state["fused"] is not None:
+                        jobs.append(state["fused"])
+                        state["fused"] = None
                     state["tile"] += 1
                     o = 0
                 state["offset"] = o

from contextlib import ExitStack

import concourse.mybir as mybir
from concourse.masks import make_identity

F32 = mybir.dt.float32
BF16 = mybir.dt.bfloat16
U32 = mybir.dt.uint32
I32 = mybir.dt.int32
U8 = mybir.dt.uint8
FP8X4 = mybir.dt.float8_e4m3fn_x4
ALU = mybir.AluOpType
ACT = mybir.ActivationFunctionType
AX = mybir.AxisListType

P = 128
FLOPS = 2 * 768 * 512 * 2048 + 2 * 2 * 2048 * 8 * 25 * 32

N_CHUNKS = 25
GROUPS = ((0, 0, 1), (0, 1, 1), (0, 2, 2), (1, 0, 4), (2, 0, 4), (3, 0, 4))
VECTOR_REDUCED = (1, 3, 6, 12, 18, 23, 24)
EVACUATIONS = (("v0", "v1"), ("v2", "v3"), ("v4", "k5"), ("k6", "k7"), ("v5", "v6", "v7"))
WARMERS = 0
FOLD_TWICE = ()
VECTOR_OFFSETS = 13
VECTOR_MULT = 0
SCALAR_BUDGET = 10
TMP_BUFS = 3
FOLD_EVERY = 99
EARLY_OFFSETS = 0
K_DEAD_LAG = 0
K_ROWS_REUSED = 2


def tile_relation_kernel(tc, x, w_qkv, out):
    nc = tc.nc
    with ExitStack() as ctx:
        ctx.enter_context(tc.manual_schedule())
        keep = ctx.enter_context(tc.tile_pool(name="keep", bufs=1))
        ring = ctx.enter_context(tc.tile_pool(name="ring", bufs=5))
        soft = ctx.enter_context(tc.tile_pool(name="soft", bufs=2))
        psum = ctx.enter_context(tc.psum_pool(name="psum", bufs=2))

        ident_f = keep.tile([P, P], F32, name="ident_f")
        make_identity(nc, ident_f[:])
        ident_b = keep.tile([P, P], BF16, name="ident_b")
        make_identity(nc, ident_b[:])
        wc = keep.tile([P, 768], U32, name="wc", align_bytes=64)
        ws = keep.tile([P, 768], U8, name="ws", align_bytes=64)
        k_rows = [keep.tile([P, 32, 64], F32, name="k%d" % r) for r in range(8)]
        v_rows = [keep.tile([P, 8, 8, 32], F32, name="v%d" % r) for r in range(8)]
        core_c = [keep.tile([P, 512], U32, name="cc%d" % r, align_bytes=64) for r in range(4)]
        core_s = [keep.tile([P, 512], U8, name="cs%d" % r, align_bytes=64) for r in range(4)]

        bank_bufs = {"w": 3, "qp": 3, "st": 2}

        def bank(shape, dtype, name, tag):
            return psum.tile(shape, dtype, name=name, tag=tag, bufs=bank_bufs[tag])

        def ring_tile(shape, dtype, name):
            return ring.tile(shape, dtype, name=name, tag="b8", align_bytes=64)

        def project(dst, codes, scales, lo, hi):
            nc.tensor.matmul_mx(
                out=dst,
                lhsT=codes.bitcast(FP8X4),
                lhsT_scale=scales,
                rhs=wc[:, lo:hi].bitcast(FP8X4),
                rhs_scale=ws[:, lo:hi],
                start=True,
                stop=True,
            )

        wraw = ring_tile([P, 6, 512], BF16, "wraw")
        nc.sync.dma_start(out=wraw[:], in_=w_qkv.rearrange("(r p) k -> p r k", p=P))
        raws = []
        for n in range(2):
            raw = ring_tile([P, 4, 1024], BF16, "raw%d" % n)
            nc.sync.dma_start(out=raw[:], in_=x[n].rearrange("(t p) h w -> p t (h w)", p=P))
            raws.append(raw)

        wgrp = ring_tile([P, 768, 4], BF16, "wgrp")
        for r in range(6):
            ty, hh = divmod(r, 2)
            wt = bank([P, 4, P], BF16, "wt", "w")
            for t in range(4):
                nc.tensor.transpose(wt[:, t, :], wraw[:, r, P * t : P * (t + 1)], ident_b[:])
            if ty < 2:
                dst = wgrp[:, 256 * ty : 256 * (ty + 1), :].rearrange("p (c h) t -> p c h t", h=8)
                dst = dst[:, :, 4 * hh : 4 * (hh + 1), :]
                src = wt[:].rearrange("p t (h c) -> p c h t", c=32)
            else:
                dst = wgrp[:, 512 + P * hh : 512 + P * (hh + 1), :]
                src = wt[:].rearrange("p t r -> p r t")
            if r % 2 == 0:
                nc.vector.tensor_copy(out=dst, in_=src)
            else:
                nc.scalar.copy(out=dst, in_=src)

        inters = []
        for n in range(2):
            inter = ring_tile([P, 1024, 4], BF16, "inter%d" % n)
            for eng, lo, hi in ((nc.vector.tensor_copy, 0, 640), (nc.scalar.copy, 640, 1024)):
                eng(
                    out=inter[:, lo:hi, :].rearrange("p (c i) t -> p c t i", i=4),
                    in_=raws[n][:, :, lo:hi].rearrange("p t (c i) -> p c t i", i=4),
                )
            inters.append(
                inter[:]
                .rearrange("p x t -> p (x t)")
                .bitcast(F32)
                .rearrange("p (hb hl wb wl u) -> p hb hl wb wl u", hb=8, hl=4, wb=8, wl=4)
            )
            if n == 0:
                for ty in range(3):
                    cols = slice(256 * ty, 256 * (ty + 1))
                    nc.vector.quantize_mx(
                        out=wc[:, cols].bitcast(FP8X4),
                        scales=ws[:, cols],
                        in_=wgrp[:, cols, :].rearrange("p w t -> p (w t)"),
                    )

        tiles = {}
        row_parts = {}

        def gather_row(a):
            grp = ring_tile([P, 4096], BF16, "grp")
            g_f = grp[:].bitcast(F32).rearrange("p (b n hb wb u) -> p b n hb wb u", b=8, n=2, hb=8, wb=8)
            nc.vector.memset(g_f[:, 0:2, :, :, 0, :], 0.0)
            nc.vector.memset(g_f[:, 6:8, :, :, 7, :], 0.0)
            for n in range(2):
                for bs, wls, wd, wsrc in (
                    (slice(0, 2), slice(2, 4), slice(1, 8), slice(0, 7)),
                    (slice(2, 6), slice(0, 4), slice(0, 8), slice(0, 8)),
                    (slice(6, 8), slice(0, 2), slice(0, 7), slice(1, 8)),
                ):
                    nc.vector.tensor_copy(
                        out=g_f[:, bs, n, :, wd, :],
                        in_=inters[n][:, :, a - 2, wsrc, wls, :].rearrange("p hb wb wl u -> p wl hb wb u"),
                    )
            return grp

        def name_tiles(a, parts):
            row_parts[a] = parts
            for b0, b1, c_ap, s_ap in parts:
                for b in range(b0, b1):
                    cols = slice(P * (b - b0), P * (b - b0 + 1))
                    tiles[(a, b)] = (c_ap[:, cols], s_ap[:, cols])

        def quantise_row(codes, a, grp):
            hc = codes.tile([P, 512], U32, name="hc%d" % a, align_bytes=64)
            hs = codes.tile([P, 512], U8, name="hs%d" % a, align_bytes=64)
            parts = (
                (0, 2, hc[:, 0:256], hs[:, 0:256]),
                (2, 6, core_c[a - 2][:], core_s[a - 2][:]),
                (6, 8, hc[:, 256:512], hs[:, 256:512]),
            )
            for b0, b1, c_ap, s_ap in parts:
                nc.vector.quantize_mx(out=c_ap.bitcast(FP8X4), scales=s_ap, in_=grp[:, 512 * b0 : 512 * b1])
            name_tiles(a, parts)

        def move_row(codes, a):
            hc = codes.tile([P, 1024], U32, name="hc%d" % a, align_bytes=64)
            hs = codes.tile([P, 1024], U8, name="hs%d" % a, align_bytes=64)
            for which, dst_t, width, sh in ((2, hc, 64, 8), (3, hs, 16, 2)):
                dst = dst_t[:].bitcast(I32).rearrange("p (m x) -> p m x", x=width)
                nc.vector.memset(dst[:, :, 0:sh] if a < 2 else dst[:, :, width - sh : width], 0)
                for part in row_parts[a + 4 if a < 2 else a - 4]:
                    src = part[which].bitcast(I32).rearrange("p (m x) -> p m x", x=width)
                    rows = slice(2 * part[0], 2 * part[1])
                    if a < 2:
                        nc.vector.tensor_copy(out=dst[:, rows, sh:width], in_=src[:, :, 0 : width - sh])
                    else:
                        nc.vector.tensor_copy(out=dst[:, rows, 0 : width - sh], in_=src[:, :, sh:width])
            name_tiles(a, ((0, 8, hc[:], hs[:]),))

        def evacuate(what, a, tags):
            for r, b0 in enumerate((0, 2, 4, 6)):
                ps = bank([P, 2, 256], F32, "ps", tags[r % len(tags)])
                for u in range(2):
                    lo = 256 if what == "k" else 512
                    project(ps[:, u, :], tiles[(a, b0 + u)][0], tiles[(a, b0 + u)][1], lo, lo + 256)
                if what == "k":
                    nc.scalar.copy(
                        out=k_rows[a][:, :, 8 * b0 : 8 * (b0 + 2)].rearrange("p c (u h) -> p c u h", h=8),
                        in_=ps[:].rearrange("p u (c h) -> p c u h", h=8),
                    )
                else:
                    nc.scalar.copy(out=v_rows[a][:, b0 : b0 + 2, :, :].rearrange("p b h c -> p b (h c)"), in_=ps[:])

        chunks = [[] for k in range(N_CHUNKS)]
        col = 0
        for gi, (hl, wl0, nt) in enumerate(GROUPS):
            for o in range(25):
                chunks[col // P].append((gi, o, col % P))
                col += 8 * nt
        max_step = {}
        for k in range(N_CHUNKS):
            for gi, o, f0 in chunks[k]:
                max_step[gi] = max(max_step.get(gi, 0), k + 2 if k in VECTOR_REDUCED else k + 4)
        K_DEAD = {}
        for k in range(N_CHUNKS):
            for gi, o, f0 in chunks[k]:
                K_DEAD[GROUPS[gi][0] + o // 5] = k + K_DEAD_LAG
        group_of_tile = {}
        for gi, (hl, wl0, nt) in enumerate(GROUPS):
            for wl in range(wl0, wl0 + nt):
                group_of_tile[4 * hl + wl] = gi

        q_banks = {}

        def q_bank(hl, ch):
            qp = bank([P, 4, 16, 8], F32, "qp", "qp")
            for wl in range(4):
                project(
                    qp[:, wl, :, :].rearrange("p c h -> p (c h)"),
                    tiles[(hl + 2, wl + 2)][0],
                    tiles[(hl + 2, wl + 2)][1],
                    P * ch,
                    P * (ch + 1),
                )
            q_banks[(hl, ch)] = qp

        def rows_of(k):
            return sorted(set(GROUPS[gi][0] for gi, o, f0 in chunks[k]))

        halves = {}

        def products(k, ch):
            cs = slice(16 * ch, 16 * (ch + 1))
            pr = ring_tile([P, 16, P], F32, "pr")
            todo = list(chunks[k])
            while todo:
                gi, o, f0 = todo[0]
                hl, wl0, nt = GROUPS[gi]
                i, j = divmod(o, 5)
                run = 1
                if nt == 1:
                    while run < len(todo) and run < 5 - j and todo[run][0] == gi:
                        run += 1
                todo = todo[run:]
                w = 8 * nt * run
                qv = q_banks[(hl, ch)][:, wl0 : wl0 + nt, :, :].rearrange("p wl c h -> p c wl h")
                if run > 1:
                    qv = qv.to_broadcast([P, 16, run, 8])
                nc.vector.tensor_tensor(
                    out=pr[:, :, f0 : f0 + w].rearrange("p c (wl h) -> p c wl h", h=8),
                    in0=qv,
                    in1=k_rows[hl + i][:, cs, 8 * (wl0 + j) : 8 * (wl0 + j) + w].rearrange("p c (wl h) -> p c wl h", h=8),
                    op=ALU.mult,
                )
            halves[(k, ch)] = pr

        def fold(k):
            a_ap = halves[(k, 0)][:].rearrange("p c f -> p (c f)")
            nc.gpsimd.tensor_tensor(out=a_ap, in0=a_ap, in1=halves[(k, 1)][:].rearrange("p c f -> p (c f)"), op=ALU.add)
            if k in FOLD_TWICE:
                nc.gpsimd.tensor_tensor(out=a_ap[:, 0:1024], in0=a_ap[:, 0:1024], in1=a_ap[:, 1024:2048], op=ALU.add)

        def left(k):
            return 8 if k in FOLD_TWICE else 16

        ssbs = {}

        def score_parts(k):
            parts = []
            for gi in sorted(set(s[0] for s in chunks[k])):
                mine = [s for s in chunks[k] if s[0] == gi]
                w = 8 * GROUPS[gi][2]
                if gi not in ssbs:
                    if w < 32:
                        ssbs[gi] = soft.tile([P, 25, w], F32, name="ssn", tag="ssn", bufs=3)
                    else:
                        ssbs[gi] = soft.tile([P, 25, w], F32, name="ssb", tag="ssb")
                parts.append((ssbs[gi][:, mine[0][1] : mine[-1][1] + 1, :], mine[0][2], mine[-1][2] + w, w))
            return parts

        def vector_reduce(k):
            for dst, f0, f1, w in score_parts(k):
                nc.vector.tensor_reduce(
                    out=dst,
                    in_=halves[(k, 0)][:, 0 : left(k), f0:f1].rearrange("p c (s f) -> p s f c", f=w),
                    axis=AX.X,
                    op=ALU.add,
                )

        sts = {}

        def warm(n):
            for r in range(n):
                dm = psum.tile([P, 512], F32, name="dm", tag="dm", bufs=1)
                project(dm[:], wc[:, 0:P], ws[:, 0:P], 256, 768)

        def tensor_reduce(k):
            st = bank([P, P], F32, "st", "st")
            for c in range(left(k)):
                nc.tensor.matmul(
                    out=st[:],
                    lhsT=halves[(k, 0)][:, c, :],
                    rhs=ident_f[:],
                    is_transpose=True,
                    start=(c == 0),
                    stop=(c == left(k) - 1),
                )
            sts[k] = st

        def copy_st(k):
            stsb = soft.tile([P, P], F32, name="stsb", tag="stsb")
            nc.scalar.copy(out=stsb[:], in_=sts[k][:])
            sts[k] = stsb

        def back(k):
            sbp = bank([P, P], F32, "sbp", "st")
            nc.tensor.transpose(sbp[:], sts[k][:], ident_f[:])
            sts[k] = sbp

        def copy_back(k):
            for dst, f0, f1, w in score_parts(k):
                nc.scalar.copy(out=dst, in_=sts[k][:, f0:f1].rearrange("p (s f) -> p s f", f=w))

        nmxs = {}
        es = {}
        sums = {}

        def softmax_max(gi):
            w = 8 * GROUPS[gi][2]
            mx = soft.tile([P, w], F32, name="mx", tag="mx")
            nc.vector.tensor_reduce(out=mx[:], in_=ssbs[gi][:].rearrange("p o f -> p f o"), axis=AX.X, op=ALU.max)
            nmx = soft.tile([P, w], F32, name="nmx", tag="nmx")
            nc.vector.tensor_scalar(out=nmx[:], in0=mx[:], scalar1=-1.0, scalar2=None, op0=ALU.mult)
            nmxs[gi] = nmx

        def softmax_exp(late, gi):
            w = 8 * GROUPS[gi][2]
            if w < 32:
                e = soft.tile([P, w, 25], F32, name="en", tag="en", bufs=3)
            else:
                e = late.tile([P, w, 25], F32, name="e", tag="e", bufs=3)
            ssum = soft.tile([P, w], F32, name="ssum", tag="ssum")
            for f in range(w):
                nc.scalar.activation(
                    out=e[:, f, :],
                    in_=ssbs[gi][:, :, f],
                    func=ACT.Exp,
                    bias=nmxs[gi][:, f : f + 1],
                    scale=1.0,
                    accum_out=ssum[:, f : f + 1],
                )
            es[gi] = e
            sums[gi] = ssum

        def softmax_norm(gi):
            w = 8 * GROUPS[gi][2]
            rs = soft.tile([P, w], F32, name="rs", tag="rs")
            nc.vector.reciprocal(out=rs[:], in_=sums[gi][:])
            nc.vector.tensor_tensor(
                out=es[gi][:], in0=es[gi][:], in1=rs[:].unsqueeze(2).to_broadcast([P, w, 25]), op=ALU.mult
            )

        def weights(hl, wl):
            gi = group_of_tile[4 * hl + wl]
            f0 = 8 * (wl - GROUPS[gi][1])
            return es[gi][:, f0 : f0 + 8, :]

        free_tags = ["tmp"] * TMP_BUFS
        freed_rows = []

        def tmp_tile(late, it):
            for a in range(8):
                if it > K_DEAD[a] and a not in freed_rows and len(freed_rows) < K_ROWS_REUSED:
                    freed_rows.append(a)
                    free_tags.append("k%d" % a)
            tag = free_tags.pop(0)
            if tag == "tmp":
                tmp = late.tile([P, 5, 8, 32], F32, name="tmp", tag="tmp", bufs=TMP_BUFS)
            else:
                tmp = keep.tile([P, 5, 8, 32], F32, name="tmk", tag=tag)
            return tmp, tag

        def piece_scalar(late, hl, wl, offsets, it):
            tmp, tag = tmp_tile(late, it)
            att = weights(hl, wl)
            for r, o in enumerate(offsets):
                for h in range(8):
                    nc.scalar.activation(
                        out=tmp[:, r, h, :],
                        in_=v_rows[hl + o // 5][:, wl + o % 5, h, :],
                        func=ACT.Copy,
                        scale=att[:, h, o : o + 1],
                    )
            return tmp, tag

        def piece_fused(late, hl, wl, offsets):
            acc = late.tile([P, 1, 8, 32], F32, name="acc", tag="acc", bufs=2)
            att = weights(hl, wl)
            for r, o in enumerate(offsets):
                for h in range(8):
                    val = v_rows[hl + o // 5][:, wl + o % 5, h, :]
                    if r == 0:
                        nc.vector.tensor_scalar(
                            out=acc[:, 0, h, :], in0=val, scalar1=att[:, h, o : o + 1], scalar2=None, op0=ALU.mult
                        )
                    else:
                        nc.vector.scalar_tensor_tensor(
                            out=acc[:, 0, h, :],
                            in0=val,
                            scalar=att[:, h, o : o + 1],
                            in1=acc[:, 0, h, :],
                            op0=ALU.mult,
                            op1=ALU.add,
                        )
            return acc

        def piece_mult(late, hl, wl, i, it):
            tmp, tag = tmp_tile(late, it)
            nc.vector.tensor_tensor(
                out=tmp[:],
                in0=v_rows[hl + i][:, wl : wl + 5, :, :],
                in1=weights(hl, wl)[:, :, 5 * i : 5 * (i + 1)]
                .rearrange("p h j -> p j h")
                .unsqueeze(3)
                .to_broadcast([P, 5, 8, 32]),
                op=ALU.mult,
            )
            return tmp, tag

        ots = {}
        done = {}

        def accumulate(late, g, wl, tmp, n_slices, n_offsets):
            if g not in ots:
                ots[g] = [bank([P, 512], F32, "ot%d" % half, "w") for half in range(2)]
            first = done.get((g, wl), 0) == 0
            done[(g, wl)] = done.get((g, wl), 0) + n_offsets
            last = done[(g, wl)] == 25
            for r in range(n_slices):
                for half in range(2):
                    nc.tensor.matmul(
                        out=ots[g][half][:, P * wl : P * (wl + 1)],
                        lhsT=tmp[:, r, 4 * half : 4 * (half + 1), :].rearrange("p h c -> p (h c)"),
                        rhs=ident_f[:],
                        is_transpose=True,
                        start=(first and r == 0),
                        stop=(last and r == n_slices - 1),
                    )
            if last and wl == 3:
                for half in range(2):
                    ost = late.tile([P, 16, 8, 4], F32, name="ost", tag="ost", bufs=2)
                    src = ots[g][half][:].rearrange("c (wl m wb) -> c m wb wl", wl=4, wb=8)
                    if half == 0:
                        nc.vector.tensor_copy(out=ost[:], in_=src)
                    else:
                        nc.scalar.copy(out=ost[:], in_=src)
                    for n in range(2):
                        nc.sync.dma_start(
                            out=out[n, P * half : P * (half + 1)].rearrange("c (hb hl) w -> c hb hl w", hl=4)[:, :, g, :],
                            in_=ost[:, 8 * n : 8 * (n + 1)].rearrange("c m wb wl -> c m (wb wl)"),
                        )

        state = {"tile": 0, "offset": 0, "made": [], "exp": [], "norm": [], "ready": -1, "fold": [], "folded": [], "fused": None}

        def step(late, it):
            k = it - 2
            on_tensor = 0 <= k < N_CHUNKS and k not in VECTOR_REDUCED
            back_due = 0 <= k - 1 < N_CHUNKS and k - 1 not in VECTOR_REDUCED
            folded = []
            for g, wl, t0, t1 in state["fold"]:
                a_ap = t0[0][:].rearrange("p j h c -> p (j h c)")
                nc.gpsimd.tensor_tensor(out=a_ap, in0=a_ap, in1=t1[0][:].rearrange("p j h c -> p (j h c)"), op=ALU.add)
                free_tags.append(t1[1])
                folded.append((g, wl, t0, 5, 10))
            state["fold"] = []
            if it + 1 < N_CHUNKS:
                for hl in rows_of(it + 1):
                    if (hl, 0) not in q_banks:
                        q_bank(hl, 0)
            if 0 <= k < N_CHUNKS and k in VECTOR_REDUCED:
                vector_reduce(k)
            for gi in range(len(GROUPS)):
                if max_step[gi] == it:
                    softmax_max(gi)
                    state["exp"].append(gi)
            if it < N_CHUNKS:
                products(it, 0)
            for gi in state["norm"]:
                softmax_norm(gi)
                state["ready"] = gi
            state["norm"] = []
            if it < N_CHUNKS:
                for hl in rows_of(it):
                    if (hl, 1) not in q_banks:
                        q_bank(hl, 1)
                products(it, 1)
                fold(it)
            made = []
            jobs = []
            budget = SCALAR_BUDGET - (5 if state["exp"] else 0)
            while late is not None and budget > 0 and state["tile"] < 16 and group_of_tile[state["tile"]] <= state["ready"]:
                g, wl = divmod(state["tile"], 4)
                o = state["offset"]
                share = VECTOR_OFFSETS if it >= N_CHUNKS else EARLY_OFFSETS
                if share and (o == 0 or (it >= N_CHUNKS and state["fused"] is None)):
                    n = ((25 - o) * share + 12) // 25
                    state["fused"] = (g, wl, None, (piece_fused(late, g, wl, list(range(o, o + n))), None), 1, n)
                    o += n
                if it >= N_CHUNKS:
                    budget = 25 - o
                n = min(5, 25 - o, budget)
                while n > 0:
                    jobs.append((g, wl, list(range(o, o + n)), None, n, n))
                    budget -= n
                    o += n
                    n = min(5, 25 - o, budget)
                if o == 25:
                    if state["fused"] is not None:
                        jobs.append(state["fused"])
                        state["fused"] = None
                    state["tile"] += 1
                    o = 0
                state["offset"] = o
                if it >= N_CHUNKS:
                    budget = 0
            if it < len(EVACUATIONS):
                for name in EVACUATIONS[it]:
                    evacuate(name[0], int(name[1]), ("w",))
            if on_tensor:
                tensor_reduce(k)
                warm(WARMERS)
            if back_due:
                back(k - 1)
            for g, wl, tmp, n_slices, n_offsets in state["folded"] + state["made"]:
                accumulate(late, g, wl, tmp[0], n_slices, n_offsets)
                if tmp[1] is not None:
                    free_tags.append(tmp[1])
                warm(WARMERS)
            state["folded"] = folded
            copies = [on_tensor, back_due]

            def small_copies():
                if copies[0]:
                    copy_st(k)
                if copies[1]:
                    copy_back(k - 1)
                copies[0] = False
                copies[1] = False

            for g, wl, offsets, tmp, n_slices, n_offsets in jobs:
                if offsets is None:
                    made.append((g, wl, tmp, n_slices, n_offsets))
                elif offsets == "mult":
                    made.append((g, wl, piece_mult(late, g, wl, 0, it), n_slices, n_offsets))
                else:
                    made.append((g, wl, piece_scalar(late, g, wl, offsets, it), n_slices, n_offsets))
                    small_copies()
            small_copies()
            for gi in state["exp"]:
                softmax_exp(late, gi)
                state["norm"].append(gi)
            state["exp"] = []
            if (
                it < N_CHUNKS
                and it % FOLD_EVERY == 0
                and len(made) == 2
                and made[0][:2] == made[1][:2]
                and made[0][3] == 5
                and made[1][3] == 5
            ):
                state["fold"].append((made[0][0], made[0][1], made[0][2], made[1][2]))
                made = []
            state["made"] = made

        with tc.tile_pool(name="codes", bufs=1) as codes:
            every = ("w", "qp", "st")
            g2 = gather_row(2)
            g4 = gather_row(4)
            quantise_row(codes, 2, g2)
            evacuate("k", 2, every)
            g5 = gather_row(5)
            quantise_row(codes, 4, g4)
            move_row(codes, 0)
            evacuate("k", 0, every)
            g3 = gather_row(3)
            quantise_row(codes, 5, g5)
            move_row(codes, 1)
            evacuate("k", 1, every)
            quantise_row(codes, 3, g3)
            evacuate("k", 3, every)
            evacuate("k", 4, every)
            q_bank(0, 0)
            move_row(codes, 6)
            move_row(codes, 7)
            for it in range(len(EVACUATIONS)):
                step(None, it)
        with tc.tile_pool(name="late", bufs=4) as late:
            it = len(EVACUATIONS)
            while state["tile"] < 16 or state["made"] or state["fold"] or state["folded"]:
                step(late, it)
                it += 1
